import numpy as np
import ml_dtypes


def mxq(x, axis, fmt="e4m3"):
    dtype, down = {"e4m3": (ml_dtypes.float8_e4m3fn, 7), "e5m2": (ml_dtypes.float8_e5m2, 14)}[fmt]
    v = np.moveaxis(np.asarray(x, np.float32).astype(ml_dtypes.bfloat16).astype(np.float64), axis, -1)
    blocks = v.reshape(v.shape[:-1] + (-1, 32))
    amax = np.abs(blocks).max(-1, keepdims=True)
    byte = np.maximum(np.where(amax > 0, np.frexp(amax)[1] - 1 + 127, 0) - down, 1)
    scale = np.exp2(byte - 127.0)
    codes = (blocks / scale).astype(np.float32).astype(dtype).astype(np.float64)
    return np.moveaxis((codes * scale).reshape(v.shape), -1, axis)


WIDE = False


def mx_kscale(k):
    if not WIDE:
        return np.ones(k)
    levels = np.array([10, -10, 5, -5, 0])
    a = np.random.permutation(np.resize(levels, k // 512 * 4)).reshape(k // 512, 4)
    idx = np.arange(k)
    return np.exp2(a[idx // 512, idx % 128 // 32])


BF16 = ml_dtypes.bfloat16


def bf(x):
    return np.asarray(x, np.float32).astype(BF16)


def f64(x):
    return np.asarray(x).astype(np.float64)


B, L, H = 1, 1024, 1024
MASK_VALUE = -3.4028234663852886e38


def setup_inputs():
    s, t = mx_kscale(H), mx_kscale(H)
    qs = np.sqrt(1.5) * H ** 0.25
    q0 = np.random.standard_normal((B, L, H)) * qs
    k0 = np.random.standard_normal((B, L, H)) * qs + q0 * (5.0 / qs ** 2)
    return {"q": bf(q0 * s), "k": bf(k0 / s),
            "x": bf(np.random.standard_normal((B, L, H)) * t),
            "Wv": bf(np.random.standard_normal((H, H)) * 2.0 / np.sqrt(H) / t[None, :]),
            "bv": bf(np.random.standard_normal(H) * 0.1)}


def reference(q, k, x, Wv, bv):
    v = (mxq(f64(x), 2, "e4m3") @ mxq(f64(Wv), 1, "e4m3").T) + f64(bv)
    a = (mxq(f64(q), 2, "e4m3") @ mxq(f64(k), 2, "e4m3").transpose(0, 2, 1)) / H
    own = np.arange(L)[:, None] == np.arange(L)[None, :]
    a = np.where(own[None, :, :], MASK_VALUE, a)
    e = np.exp(a - a.max(-1, keepdims=True))
    return (mxq(e, 2, "e4m3") @ mxq(v, 1, "e4m3")) / e.sum(-1, keepdims=True)

@@ -1,0 +1,255 @@
+from contextlib import ExitStack
+
+import concourse.bass as bass
+import concourse.mybir as mybir
+import concourse.tile as tile
+from concourse.masks import make_identity
+
+FLOPS = 3 * 2 * 1024 * 1024 * 1024
+
+F32 = mybir.dt.float32
+BF16 = mybir.dt.bfloat16
+U32 = mybir.dt.uint32
+U8 = mybir.dt.uint8
+FP8X4 = mybir.dt.float8_e4m3fn_x4
+ALU = mybir.AluOpType
+ACT = mybir.ActivationFunctionType
+AX = mybir.AxisListType
+
+P = 128
+L = 1024
+BIG = 3.4028234663852886e38
+
+
+def e_position(i_tile, j_tile):
+    if j_tile // 4 != i_tile // 4:
+        return (j_tile % 4) * P
+    if (j_tile % 4) // 2 != (i_tile % 4) // 2:
+        return 512 + (j_tile % 2) * P
+    if j_tile != i_tile:
+        return 768
+    return 896
+
+
+def tile_scaleddotproductattention_pa_kernel(tc, q, k, x, Wv, bv, out):
+    nc = tc.nc
+    with ExitStack() as ctx:
+        const = ctx.enter_context(tc.tile_pool(name="const", bufs=1))
+        rawp = ctx.enter_context(tc.tile_pool(name="rawp", bufs=1))
+        keep = ctx.enter_context(tc.tile_pool(name="keep", bufs=1))
+        gin = ctx.enter_context(tc.tile_pool(name="gin", bufs=3))
+        gvp = ctx.enter_context(tc.tile_pool(name="gvp", bufs=2))
+        gep = ctx.enter_context(tc.tile_pool(name="gep", bufs=3))
+        small = ctx.enter_context(tc.tile_pool(name="small", bufs=3))
+        outp = ctx.enter_context(tc.tile_pool(name="outp", bufs=4))
+        psum = ctx.enter_context(tc.psum_pool(name="psum", bufs=8))
+        ctx.enter_context(tc.manual_schedule())
+
+        ident_f = const.tile([P, P], F32, name="ident_f")
+        ident_b = const.tile([P, P], BF16, name="ident_b")
+        mask = const.tile([P, P], F32, name="mask")
+        ones = const.tile([P, P], BF16, name="ones")
+        brow = const.tile([P, L], BF16, name="brow")
+        bias = const.tile([P, L], F32, name="bias")
+        sums = const.tile([P, 32], F32, name="sums")
+        rsum = const.tile([P, 8], F32, name="rsum")
+        rinv = const.tile([P, 8], F32, name="rinv")
+
+        nc.vector.memset(brow[:], 0.0)
+        nc.scalar.dma_start(out=brow[0:1, :], in_=bv.rearrange("(o n) -> o n", o=1))
+        nc.vector.memset(ones[:], 1.0)
+        make_identity(nc, ident_f[:])
+        make_identity(nc, ident_b[:])
+        nc.vector.tensor_scalar(out=mask[:], in0=ident_f[:], scalar1=-2.0, scalar2=1.0,
+                                op0=ALU.mult, op1=ALU.add)
+        nc.vector.tensor_scalar(out=mask[:], in0=mask[:], scalar1=BIG, scalar2=0.0,
+                                op0=ALU.mult, op1=ALU.add)
+
+        raw = {}
+        codes = {}
+        planes = {}
+        for nm in ("k", "q", "x", "w", "v", "e"):
+            if nm in ("k", "q", "x", "w"):
+                raw[nm] = rawp.tile([P, 8 * L], BF16, name="raw_" + nm)
+            codes[nm] = keep.tile([P, 2 * L], U32, name="codes_" + nm, align_bytes=64)
+            planes[nm] = keep.tile([P, 2 * L], U8, name="planes_" + nm, align_bytes=64)
+        for nm, src in (("k", k), ("q", q), ("x", x)):
+            view = src.flatten_outer_dims().rearrange("(g p t) h -> p g (t h)", g=2, p=P, t=4)
+            for g in range(2):
+                nc.sync.dma_start(out=raw[nm][:, g * 4096:(g + 1) * 4096], in_=view[:, g, :])
+        wview = Wv.rearrange("(m p) i -> p m i", p=P)
+        for h in range(2):
+            nc.sync.dma_start(
+                out=raw["w"][:, h * 4096:(h + 1) * 4096].rearrange("p (m i) -> p m i", m=4),
+                in_=wview[:, 4 * h:4 * h + 4, :])
+        outv = out.flatten_outer_dims().rearrange("(g p t) o -> p g t o", g=2, p=P, t=4)
+
+        e_sb = [keep.tile([P, L], BF16, name="e_sb%d" % i) for i in range(8)]
+
+        def copy_on(eng, dst, src):
+            if eng == "v":
+                nc.vector.tensor_copy(out=dst, in_=src)
+            else:
+                nc.scalar.copy(out=dst, in_=src)
+
+        def quant(nm, col, width, src):
+            nc.vector.quantize_mx(out=codes[nm][:, col:col + width].bitcast(FP8X4),
+                                  scales=planes[nm][:, col:col + width], in_=src)
+
+        def mx(dst, a, acol, b, bcol, n, first, last):
+            nc.tensor.matmul_mx(out=dst,
+                                lhsT=codes[a][:, acol:acol + P].bitcast(FP8X4),
+                                lhsT_scale=planes[a][:, acol:acol + P],
+                                rhs=codes[b][:, bcol:bcol + n].bitcast(FP8X4),
+                                rhs_scale=planes[b][:, bcol:bcol + n],
+                                start=first, stop=last)
+
+        pending = []
+        flushed = [0]
+
+        def flush():
+            for idx in range(flushed[0], len(pending)):
+                pending[idx]()
+            flushed[0] = len(pending)
+
+        def in_group(nm, n0, gs, engs):
+            grp = gin.tile([P, gs * L], BF16, tag="grp", name="grp", align_bytes=64)
+            words = raw[nm][:].bitcast(F32)
+            grp_w = grp[:].bitcast(F32).rearrange("p (c r u) -> p c r u", c=2, u=2)
+            for j in range(gs):
+                n = n0 + j
+                bank = psum.tile([P, 512], F32, tag="bank", name="tin")
+                for cu in range(4):
+                    nc.tensor.transpose(bank[:, cu * P:(cu + 1) * P],
+                                        words[:, n * 512 + cu * P:n * 512 + (cu + 1) * P],
+                                        ident_f[:])
+                copy_on(engs[j], grp_w[:, :, j * P:(j + 1) * P, :],
+                        bank[:].rearrange("p (c u r) -> p c r u", c=2, u=2))
+                if j == 0:
+                    flush()
+
+            def job():
+                for c in range(2):
+                    quant(nm, c * L + n0 * P, gs * P, grp[:, c * gs * 512:(c + 1) * gs * 512])
+            pending.append(job)
+
+        def make_bias():
+            for h in range(2):
+                pb = psum.tile([P, 512], F32, tag="bank", name="pb")
+                nc.tensor.matmul(pb[:], lhsT=ones[:], rhs=brow[:, h * 512:(h + 1) * 512],
+                                 start=True, stop=True)
+                nc.vector.tensor_copy(out=bias[:, h * 512:(h + 1) * 512], in_=pb[:])
+
+        def scores(i):
+            h, pr = i // 4, (i % 4) // 2
+            bank_a = psum.tile([P, 512], F32, tag="bank", name="sc_a")
+            bank_b = psum.tile([P, 512], F32, tag="bank", name="sc_b")
+            pieces = ((bank_a, 0, (1 - h) * 512, 512),
+                      (bank_b, 0, h * 512 + (1 - pr) * 256, 256),
+                      (bank_b, 256, (i ^ 1) * P, P),
+                      (bank_b, 384, i * P, P))
+            for bank, off, col, n in pieces:
+                for c in range(2):
+                    mx(bank[:, off:off + n], "q", c * L + i * P, "k", c * L + col, n, c == 0, c == 1)
+            dm = small.tile([P, 130], F32, tag="dm", name="dm")
+            mraw = small.tile([P, 1], F32, tag="mraw", name="mraw")
+            nbias = small.tile([P, 1], F32, tag="nbias", name="nbias")
+            nc.vector.tensor_tensor(out=dm[:, 0:P], in0=bank_b[:, 384:512], in1=mask[:], op=ALU.min)
+            nc.vector.tensor_reduce(out=dm[:, 128:129], in_=bank_a[:], axis=AX.X, op=ALU.max)
+            nc.vector.tensor_reduce(out=dm[:, 129:130], in_=bank_b[:, 0:384], axis=AX.X, op=ALU.max)
+            nc.vector.tensor_reduce(out=mraw[:], in_=dm[:], axis=AX.X, op=ALU.max)
+            nc.scalar.mul(out=nbias[:], in_=mraw[:], mul=-1.0 / L)
+            for dst0, width, src, col in ((0, 512, bank_a[:], 0), (512, 384, bank_b[:, 0:384], 1),
+                                          (896, 128, dm[:, 0:P], 2)):
+                nc.scalar.activation(out=e_sb[i][:, dst0:dst0 + width], in_=src, func=ACT.Exp,
+                                     bias=nbias[:], scale=1.0 / L,
+                                     accum_out=sums[:, 4 * i + col:4 * i + col + 1])
+
+        def e_transposes(i):
+            et = psum.tile([P, L], BF16, tag="bank", name="et")
+            for j in range(8):
+                pos = e_position(i, j)
+                nc.tensor.transpose(et[:, j * P:(j + 1) * P], e_sb[i][:, pos:pos + P], ident_b[:])
+            return et
+
+        def e_evac(i, et, eng):
+            ge = gep.tile([P, L], BF16, tag="ge", name="ge", align_bytes=64)
+            copy_on(eng, ge[:].rearrange("p (g i t) -> p g i t", g=2, t=4),
+                    et[:].rearrange("p (g t i) -> p g i t", g=2, t=4))
+            return lambda: quant("e", i * 256, 256, ge[:])
+
+        def v_bank(g, o, gv):
+            vp = psum.tile([P, 512], F32, tag="bank", name="vp")
+            for t in range(4):
+                for c in range(2):
+                    mx(vp[:, t * P:(t + 1) * P], "x", c * L + (4 * g + t) * P, "w", c * L + o * P, P,
+                       c == 0, c == 1)
+            nc.vector.tensor_tensor(
+                out=gv[:, (o % 4) * 512:(o % 4 + 1) * 512].rearrange("p (o t) -> p o t", t=4),
+                in0=vp[:].rearrange("p (t o) -> p o t", t=4),
+                in1=bias[:, o * P:(o + 1) * P].unsqueeze(2).to_broadcast([P, P, 4]),
+                op=ALU.add)
+
+        def out_tile(i):
+            osb = outp.tile([P, L], F32, tag="osb", name="osb")
+            for oh in range(2):
+                op_ = psum.tile([P, 512], F32, tag="bank", name="op_")
+                for g in range(2):
+                    mx(op_[:], "e", i * 256 + g * P, "v", g * L + oh * 512, 512, g == 0, g == 1)
+                if oh == 0:
+                    nc.scalar.activation(out=osb[:, 0:512], in_=op_[:], func=ACT.Copy,
+                                         scale=rinv[:, i:i + 1])
+                else:
+                    nc.vector.tensor_scalar(out=osb[:, 512:1024], in0=op_[:],
+                                            scalar1=rinv[:, i:i + 1], scalar2=None, op0=ALU.mult)
+            nc.sync.dma_start(out=outv[:, i // 4, i % 4, :], in_=osb[:])
+
+        vsss = ("v", "s", "s", "s")
+        in_group("k", 0, 4, vsss)
+        make_bias()
+        in_group("k", 4, 4, vsss)
+        in_group("q", 0, 4, vsss)
+        in_group("q", 4, 4, vsss)
+        for i in range(8):
+            scores(i)
+            if i == 0:
+                flush()
+        nc.vector.tensor_reduce(out=rsum[:], in_=sums[:].rearrange("p (i c) -> p i c", c=4)[:, :, 0:3],
+                                axis=AX.X, op=ALU.add)
+        nc.vector.reciprocal(out=rinv[:], in_=rsum[:])
+        ssss = ("s", "s", "s", "s")
+        in_group("x", 0, 4, ssss)
+        in_group("x", 4, 4, ssss)
+        in_group("w", 0, 4, ssss)
+        in_group("w", 4, 4, ssss)
+
+        e_jobs = {}
+
+        def e_pair(i0):
+            ets = [e_transposes(i0), e_transposes(i0 + 1)]
+            for d in range(2):
+                e_jobs[i0 + d] = e_evac(i0 + d, ets[d], "s")
+
+        v_jobs = {}
+        for qd in range(4):
+            if qd < 3:
+                e_pair(2 * qd)
+            if qd == 0:
+                flush()
+            oh, g = qd // 2, qd % 2
+            gv = gvp.tile([P, 2048], BF16, tag="gv", name="gv", align_bytes=64)
+            for b in range(4):
+                v_bank(g, 4 * oh + b, gv)
+                if b == 0 and qd > 0:
+                    v_jobs[qd - 1]()
+                if b == 1 and qd < 3:
+                    e_jobs[2 * qd]()
+                if b == 3 and qd < 3:
+                    e_jobs[2 * qd + 1]()
+            v_jobs[qd] = (lambda g_=g, oh_=oh, gv_=gv: quant("v", g_ * L + oh_ * 512, 512, gv_[:]))
+        e_pair(6)
+        v_jobs[3]()
+        for i in range(8):
+            out_tile(i)
+            if i < 2:
+                e_jobs[6 + i]()

@@ -19,6 +19,12 @@ AX = mybir.AxisListType
 P = 128
 L = 1024
 BIG = 3.4028234663852886e38
+GIN_BUFS = 6
+KE = "sssssvss"
+QE0 = "svsv"
+EB = ("sv", "ss", "sv", "ss", "s", "v", "s", "s")
+TE2 = "ssss"
+LOADS = (("k", 0, 1), ("k", 1, 1), ("k", 2, 2), ("k", 4, 2), ("k", 6, 2), ("q", 0, 2), ("q", 2, 2), ("q", 4, 4), ("x", 0, 4), ("w", 0, 4), ("x", 4, 4), ("w", 4, 4))
 
 
 def e_position(i_tile, j_tile):
@@ -37,11 +43,11 @@ def tile_scaleddotproductattention_pa_kernel(tc, q, k, x, Wv, bv, out):
         const = ctx.enter_context(tc.tile_pool(name="const", bufs=1))
         rawp = ctx.enter_context(tc.tile_pool(name="rawp", bufs=1))
         keep = ctx.enter_context(tc.tile_pool(name="keep", bufs=1))
-        gin = ctx.enter_context(tc.tile_pool(name="gin", bufs=3))
+        gin = ctx.enter_context(tc.tile_pool(name="gin", bufs=GIN_BUFS))
         gvp = ctx.enter_context(tc.tile_pool(name="gvp", bufs=2))
-        gep = ctx.enter_context(tc.tile_pool(name="gep", bufs=3))
+        gep = ctx.enter_context(tc.tile_pool(name="gep", bufs=4))
         small = ctx.enter_context(tc.tile_pool(name="small", bufs=3))
-        outp = ctx.enter_context(tc.tile_pool(name="outp", bufs=4))
+        outp = ctx.enter_context(tc.tile_pool(name="outp", bufs=12))
         psum = ctx.enter_context(tc.psum_pool(name="psum", bufs=8))
         ctx.enter_context(tc.manual_schedule())
 
@@ -73,17 +79,17 @@ def tile_scaleddotproductattention_pa_kernel(tc, q, k, x, Wv, bv, out):
                 raw[nm] = rawp.tile([P, 8 * L], BF16, name="raw_" + nm)
             codes[nm] = keep.tile([P, 2 * L], U32, name="codes_" + nm, align_bytes=64)
             planes[nm] = keep.tile([P, 2 * L], U8, name="planes_" + nm, align_bytes=64)
+        views = {"w": Wv.rearrange("(m p) i -> p m i", p=P)}
         for nm, src in (("k", k), ("q", q), ("x", x)):
-            view = src.flatten_outer_dims().rearrange("(g p t) h -> p g (t h)", g=2, p=P, t=4)
-            for g in range(2):
-                nc.sync.dma_start(out=raw[nm][:, g * 4096:(g + 1) * 4096], in_=view[:, g, :])
-        wview = Wv.rearrange("(m p) i -> p m i", p=P)
-        for h in range(2):
+            views[nm] = src.flatten_outer_dims().rearrange("(g p t) h -> p g t h", g=2, p=P, t=4)
+        for nm, n0, cnt in LOADS:
+            if nm == "w":
+                rows = views[nm][:, n0:n0 + cnt, :]
+            else:
+                rows = views[nm][:, n0 // 4, n0 % 4:n0 % 4 + cnt, :]
             nc.sync.dma_start(
-                out=raw["w"][:, h * 4096:(h + 1) * 4096].rearrange("p (m i) -> p m i", m=4),
-                in_=wview[:, 4 * h:4 * h + 4, :])
+                out=raw[nm][:, n0 * L:(n0 + cnt) * L].rearrange("p (m i) -> p m i", m=cnt), in_=rows)
         outv = out.flatten_outer_dims().rearrange("(g p t) o -> p g t o", g=2, p=P, t=4)
-
         e_sb = [keep.tile([P, L], BF16, name="e_sb%d" % i) for i in range(8)]
 
         def copy_on(eng, dst, src):
@@ -104,34 +110,31 @@ def tile_scaleddotproductattention_pa_kernel(tc, q, k, x, Wv, bv, out):
                                 rhs_scale=planes[b][:, bcol:bcol + n],
                                 start=first, stop=last)
 
-        pending = []
-        flushed = [0]
+        banks = {}
+        grps = {}
 
-        def flush():
-            for idx in range(flushed[0], len(pending)):
-                pending[idx]()
-            flushed[0] = len(pending)
-
-        def in_group(nm, n0, gs, engs):
-            grp = gin.tile([P, gs * L], BF16, tag="grp", name="grp", align_bytes=64)
+        def T(nm, n):
+            bank = psum.tile([P, 512], F32, tag="bank", name="tin")
             words = raw[nm][:].bitcast(F32)
-            grp_w = grp[:].bitcast(F32).rearrange("p (c r u) -> p c r u", c=2, u=2)
-            for j in range(gs):
-                n = n0 + j
-                bank = psum.tile([P, 512], F32, tag="bank", name="tin")
-                for cu in range(4):
-                    nc.tensor.transpose(bank[:, cu * P:(cu + 1) * P],
-                                        words[:, n * 512 + cu * P:n * 512 + (cu + 1) * P],
-                                        ident_f[:])
-                copy_on(engs[j], grp_w[:, :, j * P:(j + 1) * P, :],
-                        bank[:].rearrange("p (c u r) -> p c r u", c=2, u=2))
-                if j == 0:
-                    flush()
+            for cu in range(4):
+                nc.tensor.transpose(bank[:, cu * P:(cu + 1) * P],
+                                    words[:, n * 512 + cu * P:n * 512 + (cu + 1) * P], ident_f[:])
+            banks[(nm, n)] = bank
 
-            def job():
-                for c in range(2):
-                    quant(nm, c * L + n0 * P, gs * P, grp[:, c * gs * 512:(c + 1) * gs * 512])
-            pending.append(job)
+        def E(nm, n, eng, gs=1):
+            n0 = n - n % gs
+            if n == n0:
+                grps[(nm, n0)] = gin.tile([P, gs * L], BF16, tag="grp%d" % gs, name="grp", align_bytes=64,
+                                          bufs=(6 if gs == 1 else 3))
+            grp_w = grps[(nm, n0)][:].bitcast(F32).rearrange("p (c r u) -> p c r u", c=2, u=2)
+            j = n - n0
+            copy_on(eng, grp_w[:, :, j * P:(j + 1) * P, :],
+                    banks[(nm, n)][:].rearrange("p (c u r) -> p c r u", c=2, u=2))
+
+        def Q(nm, n0, gs=1):
+            grp = grps[(nm, n0)]
+            for c in range(2):
+                quant(nm, c * L + n0 * P, gs * P, grp[:, c * gs * 512:(c + 1) * gs * 512])
 
         def make_bias():
             for h in range(2):
@@ -140,24 +143,36 @@ def tile_scaleddotproductattention_pa_kernel(tc, q, k, x, Wv, bv, out):
                                  start=True, stop=True)
                 nc.vector.tensor_copy(out=bias[:, h * 512:(h + 1) * 512], in_=pb[:])
 
-        def scores(i):
+        sm = {}
+
+        def SCp(i):
             h, pr = i // 4, (i % 4) // 2
             bank_a = psum.tile([P, 512], F32, tag="bank", name="sc_a")
             bank_b = psum.tile([P, 512], F32, tag="bank", name="sc_b")
-            pieces = ((bank_a, 0, (1 - h) * 512, 512),
-                      (bank_b, 0, h * 512 + (1 - pr) * 256, 256),
+            pieces = ((bank_b, 384, i * P, P),
                       (bank_b, 256, (i ^ 1) * P, P),
-                      (bank_b, 384, i * P, P))
+                      (bank_b, 0, h * 512 + (1 - pr) * 256, 256),
+                      (bank_a, 0, (1 - h) * 512, 512))
             for bank, off, col, n in pieces:
                 for c in range(2):
                     mx(bank[:, off:off + n], "q", c * L + i * P, "k", c * L + col, n, c == 0, c == 1)
+            banks[("a", i)] = bank_a
+            banks[("b", i)] = bank_b
+
+        def SCv(i):
+            bank_a, bank_b = banks[("a", i)], banks[("b", i)]
             dm = small.tile([P, 130], F32, tag="dm", name="dm")
             mraw = small.tile([P, 1], F32, tag="mraw", name="mraw")
-            nbias = small.tile([P, 1], F32, tag="nbias", name="nbias")
             nc.vector.tensor_tensor(out=dm[:, 0:P], in0=bank_b[:, 384:512], in1=mask[:], op=ALU.min)
-            nc.vector.tensor_reduce(out=dm[:, 128:129], in_=bank_a[:], axis=AX.X, op=ALU.max)
             nc.vector.tensor_reduce(out=dm[:, 129:130], in_=bank_b[:, 0:384], axis=AX.X, op=ALU.max)
+            nc.vector.tensor_reduce(out=dm[:, 128:129], in_=bank_a[:], axis=AX.X, op=ALU.max)
             nc.vector.tensor_reduce(out=mraw[:], in_=dm[:], axis=AX.X, op=ALU.max)
+            sm[i] = (dm, mraw)
+
+        def SCs(i):
+            bank_a, bank_b = banks[("a", i)], banks[("b", i)]
+            dm, mraw = sm[i]
+            nbias = small.tile([P, 1], F32, tag="nbias", name="nbias")
             nc.scalar.mul(out=nbias[:], in_=mraw[:], mul=-1.0 / L)
             for dst0, width, src, col in ((0, 512, bank_a[:], 0), (512, 384, bank_b[:, 0:384], 1),
                                           (896, 128, dm[:, 0:P], 2)):
@@ -165,91 +180,124 @@ def tile_scaleddotproductattention_pa_kernel(tc, q, k, x, Wv, bv, out):
                                      bias=nbias[:], scale=1.0 / L,
                                      accum_out=sums[:, 4 * i + col:4 * i + col + 1])
 
-        def e_transposes(i):
+        def TEp(i):
             et = psum.tile([P, L], BF16, tag="bank", name="et")
             for j in range(8):
                 pos = e_position(i, j)
                 nc.tensor.transpose(et[:, j * P:(j + 1) * P], e_sb[i][:, pos:pos + P], ident_b[:])
-            return et
+            banks[("et", i)] = et
 
-        def e_evac(i, et, eng):
+        def TEe(i, eng):
             ge = gep.tile([P, L], BF16, tag="ge", name="ge", align_bytes=64)
             copy_on(eng, ge[:].rearrange("p (g i t) -> p g i t", g=2, t=4),
-                    et[:].rearrange("p (g t i) -> p g i t", g=2, t=4))
-            return lambda: quant("e", i * 256, 256, ge[:])
+                    banks[("et", i)][:].rearrange("p (g t i) -> p g i t", g=2, t=4))
+            grps[("e", i)] = ge
 
-        def v_bank(g, o, gv):
+        def QE(i):
+            quant("e", i * 256, 256, grps[("e", i)][:])
+
+        def VBp(g, o):
             vp = psum.tile([P, 512], F32, tag="bank", name="vp")
             for t in range(4):
                 for c in range(2):
                     mx(vp[:, t * P:(t + 1) * P], "x", c * L + (4 * g + t) * P, "w", c * L + o * P, P,
                        c == 0, c == 1)
+            banks[("vp", g, o)] = vp
+
+        def VBe(g, o):
+            oh, b = o // 4, o % 4
+            if b == 0:
+                grps[("v", g, oh)] = gvp.tile([P, 2048], BF16, tag="gv", name="gv", align_bytes=64)
             nc.vector.tensor_tensor(
-                out=gv[:, (o % 4) * 512:(o % 4 + 1) * 512].rearrange("p (o t) -> p o t", t=4),
-                in0=vp[:].rearrange("p (t o) -> p o t", t=4),
+                out=grps[("v", g, oh)][:, b * 512:(b + 1) * 512].rearrange("p (o t) -> p o t", t=4),
+                in0=banks[("vp", g, o)][:].rearrange("p (t o) -> p o t", t=4),
                 in1=bias[:, o * P:(o + 1) * P].unsqueeze(2).to_broadcast([P, P, 4]),
                 op=ALU.add)
 
-        def out_tile(i):
-            osb = outp.tile([P, L], F32, tag="osb", name="osb")
-            for oh in range(2):
-                op_ = psum.tile([P, 512], F32, tag="bank", name="op_")
-                for g in range(2):
-                    mx(op_[:], "e", i * 256 + g * P, "v", g * L + oh * 512, 512, g == 0, g == 1)
-                if oh == 0:
-                    nc.scalar.activation(out=osb[:, 0:512], in_=op_[:], func=ACT.Copy,
-                                         scale=rinv[:, i:i + 1])
-                else:
-                    nc.vector.tensor_scalar(out=osb[:, 512:1024], in0=op_[:],
-                                            scalar1=rinv[:, i:i + 1], scalar2=None, op0=ALU.mult)
-            nc.sync.dma_start(out=outv[:, i // 4, i % 4, :], in_=osb[:])
+        def QV(g, oh):
+            quant("v", g * L + oh * 512, 512, grps[("v", g, oh)][:])
 
-        vsss = ("v", "s", "s", "s")
-        in_group("k", 0, 4, vsss)
-        make_bias()
-        in_group("k", 4, 4, vsss)
-        in_group("q", 0, 4, vsss)
-        in_group("q", 4, 4, vsss)
+        def OBp(i, oh):
+            op_ = psum.tile([P, 512], F32, tag="bank", name="op_")
+            for g in range(2):
+                mx(op_[:], "e", i * 256 + g * P, "v", g * L + oh * 512, 512, g == 0, g == 1)
+            banks[("o", i, oh)] = op_
+
+        def OBe(i, oh, eng):
+            osb = outp.tile([P, 512], F32, tag="osb", name="osb")
+            if eng == "s":
+                nc.scalar.activation(out=osb[:], in_=banks[("o", i, oh)][:], func=ACT.Copy,
+                                     scale=rinv[:, i:i + 1])
+            else:
+                nc.vector.tensor_scalar(out=osb[:], in0=banks[("o", i, oh)][:],
+                                        scalar1=rinv[:, i:i + 1], scalar2=None, op0=ALU.mult)
+            nc.sync.dma_start(out=outv[:, i // 4, i % 4, oh * 512:(oh + 1) * 512], in_=osb[:])
+
+        def row_sums():
+            nc.vector.tensor_reduce(out=rsum[:], in_=sums[:].rearrange("p (i c) -> p i c", c=4)[:, :, 0:3],
+                                    axis=AX.X, op=ALU.add)
+            nc.vector.reciprocal(out=rinv[:], in_=rsum[:])
+
+        for n in range(8):
+            T("k", n)
+            E("k", n, KE[n], 2)
+            if n == 3:
+                make_bias()
+            if n % 2 == 0 and n >= 2:
+                Q("k", n - 2, 2)
+        for n in range(4):
+            T("q", n)
+            E("q", n, QE0[n])
+            if n == 0:
+                Q("k", 6, 2)
+            else:
+                Q("q", n - 1)
+        Q("q", 3)
+        extra = [("q", n) for n in range(4, 8)] + [("x", n) for n in range(4)] + [("w", n) for n in range(4)]
+        share = (2, 2, 2, 2, 1, 1, 1, 1)
+        prev = []
+        used = 0
         for i in range(8):
-            scores(i)
-            if i == 0:
-                flush()
-        nc.vector.tensor_reduce(out=rsum[:], in_=sums[:].rearrange("p (i c) -> p i c", c=4)[:, :, 0:3],
-                                axis=AX.X, op=ALU.add)
-        nc.vector.reciprocal(out=rinv[:], in_=rsum[:])
-        ssss = ("s", "s", "s", "s")
-        in_group("x", 0, 4, ssss)
-        in_group("x", 4, 4, ssss)
-        in_group("w", 0, 4, ssss)
-        in_group("w", 4, 4, ssss)
-
-        e_jobs = {}
-
-        def e_pair(i0):
-            ets = [e_transposes(i0), e_transposes(i0 + 1)]
-            for d in range(2):
-                e_jobs[i0 + d] = e_evac(i0 + d, ets[d], "s")
-
-        v_jobs = {}
-        for qd in range(4):
-            if qd < 3:
-                e_pair(2 * qd)
-            if qd == 0:
-                flush()
-            oh, g = qd // 2, qd % 2
-            gv = gvp.tile([P, 2048], BF16, tag="gv", name="gv", align_bytes=64)
+            SCp(i)
+            now = extra[used:used + share[i]]
+            used += share[i]
+            for nm, n in now:
+                T(nm, n)
+            SCv(i)
+            for j in range(len(now)):
+                E(now[j][0], now[j][1], EB[i][j])
+            for nm, n in prev:
+                Q(nm, n)
+            prev = now
+            SCs(i)
+        for nm, n in prev:
+            Q(nm, n)
+        row_sums()
+        plan = ((tuple(("x", n) for n in range(4, 8)), 0, 0), (tuple(("w", n) for n in range(4, 8)), 1, 0), ((), 0, 1), ((), 1, 1))
+        for s in range(4):
+            tiles, g, oh = plan[s]
+            for nm, n in tiles:
+                T(nm, n)
+            TEp(2 * s)
+            TEp(2 * s + 1)
+            for nm, n in tiles:
+                E(nm, n, "s")
+            if s > 0:
+                QV(plan[s - 1][1], plan[s - 1][2])
+            for nm, n in tiles:
+                Q(nm, n)
+            TEe(2 * s, "s")
+            TEe(2 * s + 1, TE2[s])
             for b in range(4):
-                v_bank(g, 4 * oh + b, gv)
-                if b == 0 and qd > 0:
-                    v_jobs[qd - 1]()
-                if b == 1 and qd < 3:
-                    e_jobs[2 * qd]()
-                if b == 3 and qd < 3:
-                    e_jobs[2 * qd + 1]()
-            v_jobs[qd] = (lambda g_=g, oh_=oh, gv_=gv: quant("v", g_ * L + oh_ * 512, 512, gv_[:]))
-        e_pair(6)
-        v_jobs[3]()
-        for i in range(8):
-            out_tile(i)
-            if i < 2:
-                e_jobs[6 + i]()
+                VBp(g, 4 * oh + b)
+                VBe(g, 4 * oh + b)
+                if b == 1:
+                    QE(2 * s)
+                if b == 3:
+                    QE(2 * s + 1)
+        for oh in range(2):
+            for i in range(8):
+                OBp(i, oh)
+                if oh == 0 and i == 0:
+                    QV(1, 1)
+                OBe(i, oh, "sv"[i % 2])

@@ -20,11 +20,43 @@ P = 128
 L = 1024
 BIG = 3.4028234663852886e38
 GIN_BUFS = 6
-KE = "sssssvss"
-QE0 = "svsv"
-EB = ("sv", "ss", "sv", "ss", "s", "v", "s", "s")
-TE2 = "ssss"
-LOADS = (("k", 0, 1), ("k", 1, 1), ("k", 2, 2), ("k", 4, 2), ("k", 6, 2), ("q", 0, 2), ("q", 2, 2), ("q", 4, 4), ("x", 0, 4), ("w", 0, 4), ("x", 4, 4), ("w", 4, 4))
+LOADS = (("x", 0, 1), ("x", 1, 1), ("x", 2, 2), ("w", 0, 2), ("w", 2, 2), ("x", 4, 4), ("w", 4, 4), ("k", 0, 4), ("k", 4, 4), ("q", 0, 4), ("q", 4, 4))
+ORDER = (
+    ('T', 'x', 0), ('Bp',), ('T', 'x', 1), ('E', 'x', 0, 's'), ('Q', 'x', 0), ('T', 'x', 2), ('Be',),
+    ('E', 'x', 1, 's'), ('E', 'x', 2, 's'), ('T', 'x', 3), ('T', 'w', 1), ('T', 'w', 0), ('T', 'w', 3),
+    ('T', 'w', 2), ('E', 'x', 3, 's'), ('Q', 'x', 2), ('Q', 'x', 3), ('Q', 'x', 1), ('E', 'w', 1, 's'),
+    ('E', 'w', 0, 's'), ('Q', 'w', 1), ('Q', 'w', 0), ('E', 'w', 3, 's'), ('Q', 'w', 3), ('VBp', 0, 1),
+    ('E', 'w', 2, 's'), ('VBp', 0, 0), ('Q', 'w', 2), ('VBp', 0, 3), ('VBp', 0, 2), ('VBe', 0, 1),
+    ('VBe', 0, 0), ('VBe', 0, 3), ('T', 'x', 5), ('T', 'x', 6), ('VBe', 0, 2), ('T', 'w', 6), ('QV', 0, 0),
+    ('E', 'w', 6, 'v'), ('E', 'x', 5, 's'), ('E', 'x', 6, 's'), ('T', 'w', 7), ('T', 'w', 4), ('Q', 'x', 6),
+    ('T', 'w', 5), ('E', 'w', 7, 's'), ('E', 'w', 4, 's'), ('Q', 'w', 6), ('T', 'x', 7), ('T', 'x', 4),
+    ('T', 'k', 3), ('Q', 'x', 5), ('Q', 'w', 7), ('Q', 'w', 4), ('E', 'x', 7, 's'), ('T', 'k', 2),
+    ('T', 'k', 1), ('Q', 'x', 7), ('T', 'k', 0), ('E', 'k', 2, 'v'), ('E', 'k', 3, 's'), ('Q', 'k', 3),
+    ('VBp', 0, 7), ('VBp', 0, 4), ('E', 'x', 4, 's'), ('E', 'w', 5, 's'), ('Q', 'k', 2), ('Q', 'x', 4),
+    ('E', 'k', 1, 's'), ('T', 'k', 6), ('T', 'k', 5), ('VBp', 1, 2), ('VBe', 0, 7), ('T', 'k', 4),
+    ('VBe', 0, 4), ('T', 'q', 2), ('E', 'k', 0, 's'), ('E', 'k', 5, 's'), ('T', 'q', 1), ('E', 'k', 6, 's'),
+    ('T', 'q', 0), ('Q', 'k', 0), ('Q', 'k', 1), ('E', 'k', 4, 's'), ('Q', 'w', 5), ('VBe', 1, 2),
+    ('T', 'q', 3), ('Q', 'k', 6), ('Q', 'k', 5), ('T', 'k', 7), ('VBp', 1, 5), ('Q', 'k', 4),
+    ('E', 'q', 2, 's'), ('T', 'q', 6), ('E', 'q', 0, 'v'), ('E', 'q', 1, 's'), ('E', 'q', 3, 's'),
+    ('E', 'k', 7, 's'), ('Q', 'q', 0), ('Q', 'q', 2), ('VBe', 1, 5), ('E', 'q', 6, 's'), ('T', 'q', 4),
+    ('Q', 'q', 1), ('E', 'q', 4, 's'), ('Q', 'k', 7), ('Q', 'q', 3), ('T', 'q', 7), ('Q', 'q', 6),
+    ('VBp', 1, 1), ('Q', 'q', 4), ('T', 'q', 5), ('SCp', 3), ('E', 'q', 7, 's'), ('E', 'q', 5, 's'),
+    ('VBe', 1, 1), ('Q', 'q', 7), ('Q', 'q', 5), ('SCp', 6), ('SCp', 1), ('SCv', 3), ('SCv', 6), ('SCp', 5),
+    ('SCs', 3), ('SCv', 1), ('SCs', 6), ('SCs', 1), ('SCp', 7), ('SCp', 0), ('SCp', 4), ('SCv', 5),
+    ('SCs', 5), ('SCv', 7), ('SCs', 7), ('SCv', 0), ('SCp', 2), ('VBp', 1, 3), ('SCv', 2), ('SCv', 4),
+    ('SCs', 0), ('VBp', 1, 7), ('SCs', 2), ('VBe', 1, 7), ('TEp', 6), ('TEp', 0), ('VBe', 1, 3), ('TEp', 5),
+    ('TEp', 2), ('TEe', 0, 's'), ('TEp', 7), ('TEe', 6, 'v'), ('QE', 0), ('VBp', 1, 6), ('TEe', 2, 's'),
+    ('QE', 6), ('TEe', 7, 's'), ('SCs', 4), ('TEe', 5, 's'), ('QE', 2), ('VBp', 1, 0), ('VBe', 1, 6),
+    ('VBp', 0, 6), ('VBp', 0, 5), ('TEp', 1), ('TEp', 4), ('VBe', 1, 0), ('QV', 1, 0), ('QE', 7),
+    ('TEe', 4, 's'), ('RS',), ('VBp', 1, 4), ('TEe', 1, 'v'), ('OBp', 6, 0), ('OBp', 2, 0), ('QE', 1),
+    ('VBe', 1, 4), ('OBp', 0, 0), ('QE', 4), ('OBe', 2, 0, 's'), ('QE', 5), ('VBe', 0, 6), ('VBe', 0, 5),
+    ('OBp', 7, 0), ('OBe', 6, 0, 's'), ('QV', 0, 1), ('OBp', 4, 0), ('OBe', 7, 0, 's'), ('QV', 1, 1),
+    ('OBe', 4, 0, 's'), ('OBe', 0, 0, 's'), ('OBp', 5, 0), ('TEp', 3), ('OBp', 1, 0), ('OBe', 5, 0, 's'),
+    ('OBp', 4, 1), ('OBe', 1, 0, 's'), ('OBp', 1, 1), ('TEe', 3, 'v'), ('OBe', 4, 1, 's'), ('QE', 3),
+    ('OBp', 7, 1), ('OBp', 5, 1), ('OBe', 1, 1, 'v'), ('OBe', 7, 1, 's'), ('OBp', 0, 1), ('OBe', 5, 1, 's'),
+    ('OBe', 0, 1, 'v'), ('OBp', 2, 1), ('OBp', 3, 0), ('OBp', 6, 1), ('OBe', 2, 1, 's'), ('OBe', 3, 0, 'v'),
+    ('OBp', 3, 1), ('OBe', 6, 1, 's'), ('OBe', 3, 1, 's'),
+)
 
 
 def e_position(i_tile, j_tile):
@@ -44,8 +76,8 @@ def tile_scaleddotproductattention_pa_kernel(tc, q, k, x, Wv, bv, out):
         rawp = ctx.enter_context(tc.tile_pool(name="rawp", bufs=1))
         keep = ctx.enter_context(tc.tile_pool(name="keep", bufs=1))
         gin = ctx.enter_context(tc.tile_pool(name="gin", bufs=GIN_BUFS))
-        gvp = ctx.enter_context(tc.tile_pool(name="gvp", bufs=2))
-        gep = ctx.enter_context(tc.tile_pool(name="gep", bufs=4))
+        gvp = ctx.enter_context(tc.tile_pool(name="gvp", bufs=4))
+        gep = ctx.enter_context(tc.tile_pool(name="gep", bufs=8))
         small = ctx.enter_context(tc.tile_pool(name="small", bufs=3))
         outp = ctx.enter_context(tc.tile_pool(name="outp", bufs=12))
         psum = ctx.enter_context(tc.psum_pool(name="psum", bufs=8))
@@ -136,12 +168,16 @@ def tile_scaleddotproductattention_pa_kernel(tc, q, k, x, Wv, bv, out):
             for c in range(2):
                 quant(nm, c * L + n0 * P, gs * P, grp[:, c * gs * 512:(c + 1) * gs * 512])
 
-        def make_bias():
+        def Bp():
             for h in range(2):
                 pb = psum.tile([P, 512], F32, tag="bank", name="pb")
                 nc.tensor.matmul(pb[:], lhsT=ones[:], rhs=brow[:, h * 512:(h + 1) * 512],
                                  start=True, stop=True)
-                nc.vector.tensor_copy(out=bias[:, h * 512:(h + 1) * 512], in_=pb[:])
+                banks[("pb", h)] = pb
+
+        def Be():
+            for h in range(2):
+                nc.vector.tensor_copy(out=bias[:, h * 512:(h + 1) * 512], in_=banks[("pb", h)][:])
 
         sm = {}
 
@@ -206,7 +242,7 @@ def tile_scaleddotproductattention_pa_kernel(tc, q, k, x, Wv, bv, out):
 
         def VBe(g, o):
             oh, b = o // 4, o % 4
-            if b == 0:
+            if ("v", g, oh) not in grps:
                 grps[("v", g, oh)] = gvp.tile([P, 2048], BF16, tag="gv", name="gv", align_bytes=64)
             nc.vector.tensor_tensor(
                 out=grps[("v", g, oh)][:, b * 512:(b + 1) * 512].rearrange("p (o t) -> p o t", t=4),
@@ -238,66 +274,7 @@ def tile_scaleddotproductattention_pa_kernel(tc, q, k, x, Wv, bv, out):
                                     axis=AX.X, op=ALU.add)
             nc.vector.reciprocal(out=rinv[:], in_=rsum[:])
 
-        for n in range(8):
-            T("k", n)
-            E("k", n, KE[n], 2)
-            if n == 3:
-                make_bias()
-            if n % 2 == 0 and n >= 2:
-                Q("k", n - 2, 2)
-        for n in range(4):
-            T("q", n)
-            E("q", n, QE0[n])
-            if n == 0:
-                Q("k", 6, 2)
-            else:
-                Q("q", n - 1)
-        Q("q", 3)
-        extra = [("q", n) for n in range(4, 8)] + [("x", n) for n in range(4)] + [("w", n) for n in range(4)]
-        share = (2, 2, 2, 2, 1, 1, 1, 1)
-        prev = []
-        used = 0
-        for i in range(8):
-            SCp(i)
-            now = extra[used:used + share[i]]
-            used += share[i]
-            for nm, n in now:
-                T(nm, n)
-            SCv(i)
-            for j in range(len(now)):
-                E(now[j][0], now[j][1], EB[i][j])
-            for nm, n in prev:
-                Q(nm, n)
-            prev = now
-            SCs(i)
-        for nm, n in prev:
-            Q(nm, n)
-        row_sums()
-        plan = ((tuple(("x", n) for n in range(4, 8)), 0, 0), (tuple(("w", n) for n in range(4, 8)), 1, 0), ((), 0, 1), ((), 1, 1))
-        for s in range(4):
-            tiles, g, oh = plan[s]
-            for nm, n in tiles:
-                T(nm, n)
-            TEp(2 * s)
-            TEp(2 * s + 1)
-            for nm, n in tiles:
-                E(nm, n, "s")
-            if s > 0:
-                QV(plan[s - 1][1], plan[s - 1][2])
-            for nm, n in tiles:
-                Q(nm, n)
-            TEe(2 * s, "s")
-            TEe(2 * s + 1, TE2[s])
-            for b in range(4):
-                VBp(g, 4 * oh + b)
-                VBe(g, 4 * oh + b)
-                if b == 1:
-                    QE(2 * s)
-                if b == 3:
-                    QE(2 * s + 1)
-        for oh in range(2):
-            for i in range(8):
-                OBp(i, oh)
-                if oh == 0 and i == 0:
-                    QV(1, 1)
-                OBe(i, oh, "sv"[i % 2])
+        acts = {"T": T, "E": E, "Q": Q, "Bp": Bp, "Be": Be, "SCp": SCp, "SCv": SCv, "SCs": SCs, "TEp": TEp, "TEe": TEe,
+                "QE": QE, "VBp": VBp, "VBe": VBe, "QV": QV, "OBp": OBp, "OBe": OBe, "RS": row_sums}
+        for step in ORDER:
+            acts[step[0]](*step[1:])

@@ -1,8 +1,6 @@
 from contextlib import ExitStack
 
-import concourse.bass as bass
 import concourse.mybir as mybir
-import concourse.tile as tile
 from concourse.masks import make_identity
 
 FLOPS = 3 * 2 * 1024 * 1024 * 1024
@@ -18,263 +16,285 @@ AX = mybir.AxisListType
 
 P = 128
 L = 1024
-BIG = 3.4028234663852886e38
-GIN_BUFS = 6
-LOADS = (("x", 0, 1), ("x", 1, 1), ("x", 2, 2), ("w", 0, 2), ("w", 2, 2), ("x", 4, 4), ("w", 4, 4), ("k", 0, 4), ("k", 4, 4), ("q", 0, 4), ("q", 4, 4))
-ORDER = (
-    ('T', 'x', 0), ('Bp',), ('T', 'x', 1), ('E', 'x', 0, 's'), ('Q', 'x', 0), ('T', 'x', 2), ('Be',),
-    ('E', 'x', 1, 's'), ('E', 'x', 2, 's'), ('T', 'x', 3), ('T', 'w', 1), ('T', 'w', 0), ('T', 'w', 3),
-    ('T', 'w', 2), ('E', 'x', 3, 's'), ('Q', 'x', 2), ('Q', 'x', 3), ('Q', 'x', 1), ('E', 'w', 1, 's'),
-    ('E', 'w', 0, 's'), ('Q', 'w', 1), ('Q', 'w', 0), ('E', 'w', 3, 's'), ('Q', 'w', 3), ('VBp', 0, 1),
-    ('E', 'w', 2, 's'), ('VBp', 0, 0), ('Q', 'w', 2), ('VBp', 0, 3), ('VBp', 0, 2), ('VBe', 0, 1),
-    ('VBe', 0, 0), ('VBe', 0, 3), ('T', 'x', 5), ('T', 'x', 6), ('VBe', 0, 2), ('T', 'w', 6), ('QV', 0, 0),
-    ('E', 'w', 6, 'v'), ('E', 'x', 5, 's'), ('E', 'x', 6, 's'), ('T', 'w', 7), ('T', 'w', 4), ('Q', 'x', 6),
-    ('T', 'w', 5), ('E', 'w', 7, 's'), ('E', 'w', 4, 's'), ('Q', 'w', 6), ('T', 'x', 7), ('T', 'x', 4),
-    ('T', 'k', 3), ('Q', 'x', 5), ('Q', 'w', 7), ('Q', 'w', 4), ('E', 'x', 7, 's'), ('T', 'k', 2),
-    ('T', 'k', 1), ('Q', 'x', 7), ('T', 'k', 0), ('E', 'k', 2, 'v'), ('E', 'k', 3, 's'), ('Q', 'k', 3),
-    ('VBp', 0, 7), ('VBp', 0, 4), ('E', 'x', 4, 's'), ('E', 'w', 5, 's'), ('Q', 'k', 2), ('Q', 'x', 4),
-    ('E', 'k', 1, 's'), ('T', 'k', 6), ('T', 'k', 5), ('VBp', 1, 2), ('VBe', 0, 7), ('T', 'k', 4),
-    ('VBe', 0, 4), ('T', 'q', 2), ('E', 'k', 0, 's'), ('E', 'k', 5, 's'), ('T', 'q', 1), ('E', 'k', 6, 's'),
-    ('T', 'q', 0), ('Q', 'k', 0), ('Q', 'k', 1), ('E', 'k', 4, 's'), ('Q', 'w', 5), ('VBe', 1, 2),
-    ('T', 'q', 3), ('Q', 'k', 6), ('Q', 'k', 5), ('T', 'k', 7), ('VBp', 1, 5), ('Q', 'k', 4),
-    ('E', 'q', 2, 's'), ('T', 'q', 6), ('E', 'q', 0, 'v'), ('E', 'q', 1, 's'), ('E', 'q', 3, 's'),
-    ('E', 'k', 7, 's'), ('Q', 'q', 0), ('Q', 'q', 2), ('VBe', 1, 5), ('E', 'q', 6, 's'), ('T', 'q', 4),
-    ('Q', 'q', 1), ('E', 'q', 4, 's'), ('Q', 'k', 7), ('Q', 'q', 3), ('T', 'q', 7), ('Q', 'q', 6),
-    ('VBp', 1, 1), ('Q', 'q', 4), ('T', 'q', 5), ('SCp', 3), ('E', 'q', 7, 's'), ('E', 'q', 5, 's'),
-    ('VBe', 1, 1), ('Q', 'q', 7), ('Q', 'q', 5), ('SCp', 6), ('SCp', 1), ('SCv', 3), ('SCv', 6), ('SCp', 5),
-    ('SCs', 3), ('SCv', 1), ('SCs', 6), ('SCs', 1), ('SCp', 7), ('SCp', 0), ('SCp', 4), ('SCv', 5),
-    ('SCs', 5), ('SCv', 7), ('SCs', 7), ('SCv', 0), ('SCp', 2), ('VBp', 1, 3), ('SCv', 2), ('SCv', 4),
-    ('SCs', 0), ('VBp', 1, 7), ('SCs', 2), ('VBe', 1, 7), ('TEp', 6), ('TEp', 0), ('VBe', 1, 3), ('TEp', 5),
-    ('TEp', 2), ('TEe', 0, 's'), ('TEp', 7), ('TEe', 6, 'v'), ('QE', 0), ('VBp', 1, 6), ('TEe', 2, 's'),
-    ('QE', 6), ('TEe', 7, 's'), ('SCs', 4), ('TEe', 5, 's'), ('QE', 2), ('VBp', 1, 0), ('VBe', 1, 6),
-    ('VBp', 0, 6), ('VBp', 0, 5), ('TEp', 1), ('TEp', 4), ('VBe', 1, 0), ('QV', 1, 0), ('QE', 7),
-    ('TEe', 4, 's'), ('RS',), ('VBp', 1, 4), ('TEe', 1, 'v'), ('OBp', 6, 0), ('OBp', 2, 0), ('QE', 1),
-    ('VBe', 1, 4), ('OBp', 0, 0), ('QE', 4), ('OBe', 2, 0, 's'), ('QE', 5), ('VBe', 0, 6), ('VBe', 0, 5),
-    ('OBp', 7, 0), ('OBe', 6, 0, 's'), ('QV', 0, 1), ('OBp', 4, 0), ('OBe', 7, 0, 's'), ('QV', 1, 1),
-    ('OBe', 4, 0, 's'), ('OBe', 0, 0, 's'), ('OBp', 5, 0), ('TEp', 3), ('OBp', 1, 0), ('OBe', 5, 0, 's'),
-    ('OBp', 4, 1), ('OBe', 1, 0, 's'), ('OBp', 1, 1), ('TEe', 3, 'v'), ('OBe', 4, 1, 's'), ('QE', 3),
-    ('OBp', 7, 1), ('OBp', 5, 1), ('OBe', 1, 1, 'v'), ('OBe', 7, 1, 's'), ('OBp', 0, 1), ('OBe', 5, 1, 's'),
-    ('OBe', 0, 1, 'v'), ('OBp', 2, 1), ('OBp', 3, 0), ('OBp', 6, 1), ('OBe', 2, 1, 's'), ('OBe', 3, 0, 'v'),
-    ('OBp', 3, 1), ('OBe', 6, 1, 's'), ('OBe', 3, 1, 's'),
-)
+TILES = L // P
+BANK = 512
+MASKED = -3.4028234663852886e38
+
+LOADS = (("k", 0, 1), ("k", 1, 1), ("k", 2, 2), ("k", 4, 2), ("k", 6, 2), ("q", 0, 2), ("q", 2, 2), ("q", 4, 4),
+         ("x", 0, 4), ("w", 0, 4), ("x", 4, 4), ("w", 4, 4))
+E_TILES_BEFORE_QUARTER = ((), (0, 1, 2), (3, 4, 5), (6, 7))
+OUT_BANKS_PER_VECTOR_TURN = 4
 
 
-def e_position(i_tile, j_tile):
-    if j_tile // 4 != i_tile // 4:
-        return (j_tile % 4) * P
-    if (j_tile % 4) // 2 != (i_tile % 4) // 2:
-        return 512 + (j_tile % 2) * P
-    if j_tile != i_tile:
-        return 768
-    return 896
+def e_column(i, j):
+    if j // 4 != i // 4:
+        return (j % 4) * P
+    if (j % 4) // 2 != (i % 4) // 2:
+        return BANK + (j % 2) * P
+    if j != i:
+        return BANK + 2 * P
+    return BANK + 3 * P
 
 
 def tile_scaleddotproductattention_pa_kernel(tc, q, k, x, Wv, bv, out):
     nc = tc.nc
     with ExitStack() as ctx:
         const = ctx.enter_context(tc.tile_pool(name="const", bufs=1))
-        rawp = ctx.enter_context(tc.tile_pool(name="rawp", bufs=1))
         keep = ctx.enter_context(tc.tile_pool(name="keep", bufs=1))
-        gin = ctx.enter_context(tc.tile_pool(name="gin", bufs=GIN_BUFS))
-        gvp = ctx.enter_context(tc.tile_pool(name="gvp", bufs=4))
-        gep = ctx.enter_context(tc.tile_pool(name="gep", bufs=8))
+        to_quantise = ctx.enter_context(tc.tile_pool(name="to_quantise", bufs=6))
+        v_to_quantise = ctx.enter_context(tc.tile_pool(name="v_to_quantise", bufs=2))
         small = ctx.enter_context(tc.tile_pool(name="small", bufs=3))
-        outp = ctx.enter_context(tc.tile_pool(name="outp", bufs=12))
+        stores = ctx.enter_context(tc.tile_pool(name="stores", bufs=12))
         psum = ctx.enter_context(tc.psum_pool(name="psum", bufs=8))
         ctx.enter_context(tc.manual_schedule())
 
-        ident_f = const.tile([P, P], F32, name="ident_f")
-        ident_b = const.tile([P, P], BF16, name="ident_b")
-        mask = const.tile([P, P], F32, name="mask")
+        ident_f32 = const.tile([P, P], F32, name="ident_f32")
+        ident_bf16 = const.tile([P, P], BF16, name="ident_bf16")
+        diag_mask = const.tile([P, P], F32, name="diag_mask")
         ones = const.tile([P, P], BF16, name="ones")
-        brow = const.tile([P, L], BF16, name="brow")
+        bias_row = const.tile([P, L], BF16, name="bias_row")
         bias = const.tile([P, L], F32, name="bias")
-        sums = const.tile([P, 32], F32, name="sums")
-        rsum = const.tile([P, 8], F32, name="rsum")
-        rinv = const.tile([P, 8], F32, name="rinv")
+        part_sums = const.tile([P, 4 * TILES], F32, name="part_sums")
+        row_sum = const.tile([P, TILES], F32, name="row_sum")
+        row_scale = const.tile([P, TILES], F32, name="row_scale")
 
-        nc.vector.memset(brow[:], 0.0)
-        nc.scalar.dma_start(out=brow[0:1, :], in_=bv.rearrange("(o n) -> o n", o=1))
+        nc.vector.memset(bias_row[:], 0.0)
+        nc.scalar.dma_start(out=bias_row[0:1, :], in_=bv.rearrange("(o n) -> o n", o=1))
         nc.vector.memset(ones[:], 1.0)
-        make_identity(nc, ident_f[:])
-        make_identity(nc, ident_b[:])
-        nc.vector.tensor_scalar(out=mask[:], in0=ident_f[:], scalar1=-2.0, scalar2=1.0,
+        make_identity(nc, ident_f32[:])
+        make_identity(nc, ident_bf16[:])
+        nc.vector.tensor_scalar(out=diag_mask[:], in0=ident_f32[:], scalar1=-2.0, scalar2=1.0,
                                 op0=ALU.mult, op1=ALU.add)
-        nc.vector.tensor_scalar(out=mask[:], in0=mask[:], scalar1=BIG, scalar2=0.0,
+        nc.vector.tensor_scalar(out=diag_mask[:], in0=diag_mask[:], scalar1=-MASKED, scalar2=0.0,
                                 op0=ALU.mult, op1=ALU.add)
 
         raw = {}
-        codes = {}
-        planes = {}
-        for nm in ("k", "q", "x", "w", "v", "e"):
-            if nm in ("k", "q", "x", "w"):
-                raw[nm] = rawp.tile([P, 8 * L], BF16, name="raw_" + nm)
-            codes[nm] = keep.tile([P, 2 * L], U32, name="codes_" + nm, align_bytes=64)
-            planes[nm] = keep.tile([P, 2 * L], U8, name="planes_" + nm, align_bytes=64)
-        views = {"w": Wv.rearrange("(m p) i -> p m i", p=P)}
-        for nm, src in (("k", k), ("q", q), ("x", x)):
-            views[nm] = src.flatten_outer_dims().rearrange("(g p t) h -> p g t h", g=2, p=P, t=4)
-        for nm, n0, cnt in LOADS:
-            if nm == "w":
-                rows = views[nm][:, n0:n0 + cnt, :]
+        words = {}
+        scales = {}
+        for name in ("k", "q", "x", "w", "v", "e"):
+            if name in ("k", "q", "x", "w"):
+                raw[name] = keep.tile([P, TILES * L], BF16, name="raw_" + name)
+            words[name] = keep.tile([P, 2 * L], U32, name="words_" + name, align_bytes=64)
+            scales[name] = keep.tile([P, 2 * L], U8, name="scales_" + name, align_bytes=64)
+        e_rows = [keep.tile([P, L], BF16, name="e_rows%d" % i) for i in range(TILES)]
+
+        dram = {"w": Wv.rearrange("(n p) h -> p n h", p=P)}
+        for name, src in (("k", k), ("q", q), ("x", x)):
+            dram[name] = src.flatten_outer_dims().rearrange("(g p t) h -> p g t h", g=2, p=P, t=4)
+        for name, n0, count in LOADS:
+            if name == "w":
+                rows = dram[name][:, n0:n0 + count, :]
             else:
-                rows = views[nm][:, n0 // 4, n0 % 4:n0 % 4 + cnt, :]
-            nc.sync.dma_start(
-                out=raw[nm][:, n0 * L:(n0 + cnt) * L].rearrange("p (m i) -> p m i", m=cnt), in_=rows)
-        outv = out.flatten_outer_dims().rearrange("(g p t) o -> p g t o", g=2, p=P, t=4)
-        e_sb = [keep.tile([P, L], BF16, name="e_sb%d" % i) for i in range(8)]
+                rows = dram[name][:, n0 // 4, n0 % 4:n0 % 4 + count, :]
+            nc.sync.dma_start(out=raw[name][:, n0 * L:(n0 + count) * L].rearrange("p (n h) -> p n h", n=count),
+                              in_=rows)
+        out_rows = out.flatten_outer_dims().rearrange("(g p t) o -> p g t o", g=2, p=P, t=4)
 
-        def copy_on(eng, dst, src):
-            if eng == "v":
-                nc.vector.tensor_copy(out=dst, in_=src)
-            else:
-                nc.scalar.copy(out=dst, in_=src)
+        def first_word(name, n, c):
+            if name == "k":
+                return c * L + n * P
+            return n * 2 * P + c * P
 
-        def quant(nm, col, width, src):
-            nc.vector.quantize_mx(out=codes[nm][:, col:col + width].bitcast(FP8X4),
-                                  scales=planes[nm][:, col:col + width], in_=src)
+        def quantise(name, start, count, values):
+            nc.vector.quantize_mx(out=words[name][:, start:start + count].bitcast(FP8X4),
+                                  scales=scales[name][:, start:start + count], in_=values)
 
-        def mx(dst, a, acol, b, bcol, n, first, last):
-            nc.tensor.matmul_mx(out=dst,
-                                lhsT=codes[a][:, acol:acol + P].bitcast(FP8X4),
-                                lhsT_scale=planes[a][:, acol:acol + P],
-                                rhs=codes[b][:, bcol:bcol + n].bitcast(FP8X4),
-                                rhs_scale=planes[b][:, bcol:bcol + n],
+        def mx_pass(acc, stationary, s_start, moving, m_start, n, first, last):
+            nc.tensor.matmul_mx(out=acc,
+                                lhsT=words[stationary][:, s_start:s_start + P].bitcast(FP8X4),
+                                lhsT_scale=scales[stationary][:, s_start:s_start + P],
+                                rhs=words[moving][:, m_start:m_start + n].bitcast(FP8X4),
+                                rhs_scale=scales[moving][:, m_start:m_start + n],
                                 start=first, stop=last)
 
         banks = {}
-        grps = {}
+        grouped = {}
 
-        def T(nm, n):
-            bank = psum.tile([P, 512], F32, tag="bank", name="tin")
-            words = raw[nm][:].bitcast(F32)
+        def flip(name, n):
+            bank = psum.tile([P, BANK], F32, tag="bank", name="flipped")
+            pairs = raw[name][:].bitcast(F32)
             for cu in range(4):
                 nc.tensor.transpose(bank[:, cu * P:(cu + 1) * P],
-                                    words[:, n * 512 + cu * P:n * 512 + (cu + 1) * P], ident_f[:])
-            banks[(nm, n)] = bank
+                                    pairs[:, n * BANK + cu * P:n * BANK + (cu + 1) * P], ident_f32[:])
+            banks[(name, n)] = bank
 
-        def E(nm, n, eng, gs=1):
-            n0 = n - n % gs
-            if n == n0:
-                grps[(nm, n0)] = gin.tile([P, gs * L], BF16, tag="grp%d" % gs, name="grp", align_bytes=64,
-                                          bufs=(6 if gs == 1 else 3))
-            grp_w = grps[(nm, n0)][:].bitcast(F32).rearrange("p (c r u) -> p c r u", c=2, u=2)
-            j = n - n0
-            copy_on(eng, grp_w[:, :, j * P:(j + 1) * P, :],
-                    banks[(nm, n)][:].rearrange("p (c u r) -> p c r u", c=2, u=2))
+        def regroup(name, n):
+            tile = to_quantise.tile([P, L], BF16, tag="grouped", name="grouped", align_bytes=64)
+            nc.scalar.copy(out=tile[:].bitcast(F32).rearrange("p (c r u) -> p c r u", c=2, u=2),
+                           in_=banks[(name, n)][:].rearrange("p (c u r) -> p c r u", c=2, u=2))
+            grouped[(name, n)] = tile
 
-        def Q(nm, n0, gs=1):
-            grp = grps[(nm, n0)]
-            for c in range(2):
-                quant(nm, c * L + n0 * P, gs * P, grp[:, c * gs * 512:(c + 1) * gs * 512])
-
-        def Bp():
-            for h in range(2):
-                pb = psum.tile([P, 512], F32, tag="bank", name="pb")
-                nc.tensor.matmul(pb[:], lhsT=ones[:], rhs=brow[:, h * 512:(h + 1) * 512],
-                                 start=True, stop=True)
-                banks[("pb", h)] = pb
-
-        def Be():
-            for h in range(2):
-                nc.vector.tensor_copy(out=bias[:, h * 512:(h + 1) * 512], in_=banks[("pb", h)][:])
-
-        sm = {}
-
-        def SCp(i):
-            h, pr = i // 4, (i % 4) // 2
-            bank_a = psum.tile([P, 512], F32, tag="bank", name="sc_a")
-            bank_b = psum.tile([P, 512], F32, tag="bank", name="sc_b")
-            pieces = ((bank_b, 384, i * P, P),
-                      (bank_b, 256, (i ^ 1) * P, P),
-                      (bank_b, 0, h * 512 + (1 - pr) * 256, 256),
-                      (bank_a, 0, (1 - h) * 512, 512))
-            for bank, off, col, n in pieces:
+        def quantise_input(name, n):
+            tile = grouped[(name, n)]
+            if name == "k":
                 for c in range(2):
-                    mx(bank[:, off:off + n], "q", c * L + i * P, "k", c * L + col, n, c == 0, c == 1)
-            banks[("a", i)] = bank_a
-            banks[("b", i)] = bank_b
+                    quantise(name, first_word(name, n, c), P, tile[:, c * BANK:(c + 1) * BANK])
+            else:
+                quantise(name, first_word(name, n, 0), 2 * P, tile[:])
 
-        def SCv(i):
-            bank_a, bank_b = banks[("a", i)], banks[("b", i)]
-            dm = small.tile([P, 130], F32, tag="dm", name="dm")
-            mraw = small.tile([P, 1], F32, tag="mraw", name="mraw")
-            nc.vector.tensor_tensor(out=dm[:, 0:P], in0=bank_b[:, 384:512], in1=mask[:], op=ALU.min)
-            nc.vector.tensor_reduce(out=dm[:, 129:130], in_=bank_b[:, 0:384], axis=AX.X, op=ALU.max)
-            nc.vector.tensor_reduce(out=dm[:, 128:129], in_=bank_a[:], axis=AX.X, op=ALU.max)
-            nc.vector.tensor_reduce(out=mraw[:], in_=dm[:], axis=AX.X, op=ALU.max)
-            sm[i] = (dm, mraw)
+        def spread_bias():
+            for half in range(2):
+                bank = psum.tile([P, BANK], F32, tag="bank", name="bias_bank")
+                nc.tensor.matmul(bank[:], lhsT=ones[:], rhs=bias_row[:, half * BANK:(half + 1) * BANK],
+                                 start=True, stop=True)
+                nc.vector.tensor_copy(out=bias[:, half * BANK:(half + 1) * BANK], in_=bank[:])
 
-        def SCs(i):
-            bank_a, bank_b = banks[("a", i)], banks[("b", i)]
-            dm, mraw = sm[i]
-            nbias = small.tile([P, 1], F32, tag="nbias", name="nbias")
-            nc.scalar.mul(out=nbias[:], in_=mraw[:], mul=-1.0 / L)
-            for dst0, width, src, col in ((0, 512, bank_a[:], 0), (512, 384, bank_b[:, 0:384], 1),
-                                          (896, 128, dm[:, 0:P], 2)):
-                nc.scalar.activation(out=e_sb[i][:, dst0:dst0 + width], in_=src, func=ACT.Exp,
-                                     bias=nbias[:], scale=1.0 / L,
-                                     accum_out=sums[:, 4 * i + col:4 * i + col + 1])
+        def scores(i):
+            half, pair = i // 4, (i % 4) // 2
+            own = psum.tile([P, BANK], F32, tag="bank", name="own_half")
+            other = psum.tile([P, BANK], F32, tag="bank", name="other_half")
+            for bank, column, key_tile, n in ((own, 3 * P, i, P), (own, 2 * P, i ^ 1, P),
+                                              (own, 0, 4 * half + 2 * (1 - pair), 2 * P),
+                                              (other, 0, 4 * (1 - half), BANK)):
+                for c in range(2):
+                    mx_pass(bank[:, column:column + n], "q", first_word("q", i, c), "k", first_word("k", key_tile, c),
+                            n, c == 0, c == 1)
+            banks[("own", i)] = own
+            banks[("other", i)] = other
 
-        def TEp(i):
-            et = psum.tile([P, L], BF16, tag="bank", name="et")
-            for j in range(8):
-                pos = e_position(i, j)
-                nc.tensor.transpose(et[:, j * P:(j + 1) * P], e_sb[i][:, pos:pos + P], ident_b[:])
-            banks[("et", i)] = et
+        def row_max(i):
+            diag = small.tile([P, P + 2], F32, tag="diag", name="diag")
+            top = small.tile([P, 1], F32, tag="top", name="top")
+            own, other = banks[("own", i)], banks[("other", i)]
+            nc.vector.tensor_tensor(out=diag[:, 0:P], in0=own[:, 3 * P:BANK], in1=diag_mask[:], op=ALU.min)
+            nc.vector.tensor_reduce(out=diag[:, P + 1:P + 2], in_=own[:, 0:3 * P], axis=AX.X, op=ALU.max)
+            nc.vector.tensor_reduce(out=diag[:, P:P + 1], in_=other[:], axis=AX.X, op=ALU.max)
+            nc.vector.tensor_reduce(out=top[:], in_=diag[:], axis=AX.X, op=ALU.max)
+            grouped[("diag", i)] = diag
+            grouped[("top", i)] = top
 
-        def TEe(i, eng):
-            ge = gep.tile([P, L], BF16, tag="ge", name="ge", align_bytes=64)
-            copy_on(eng, ge[:].rearrange("p (g i t) -> p g i t", g=2, t=4),
-                    banks[("et", i)][:].rearrange("p (g t i) -> p g i t", g=2, t=4))
-            grps[("e", i)] = ge
+        def exponentials(i):
+            shift = small.tile([P, 1], F32, tag="shift", name="shift")
+            nc.scalar.mul(out=shift[:], in_=grouped[("top", i)][:], mul=-1.0 / L)
+            for part, column, n, src in ((0, 0, BANK, banks[("other", i)][:]),
+                                         (1, BANK, 3 * P, banks[("own", i)][:, 0:3 * P]),
+                                         (2, BANK + 3 * P, P, grouped[("diag", i)][:, 0:P])):
+                nc.scalar.activation(out=e_rows[i][:, column:column + n], in_=src, func=ACT.Exp,
+                                     bias=shift[:], scale=1.0 / L,
+                                     accum_out=part_sums[:, 4 * i + part:4 * i + part + 1])
 
-        def QE(i):
-            quant("e", i * 256, 256, grps[("e", i)][:])
+        def row_scales():
+            nc.vector.tensor_reduce(out=row_sum[:], in_=part_sums[:].rearrange("p (i m) -> p i m", m=4)[:, :, 0:3],
+                                    axis=AX.X, op=ALU.add)
+            nc.vector.reciprocal(out=row_scale[:], in_=row_sum[:])
 
-        def VBp(g, o):
-            vp = psum.tile([P, 512], F32, tag="bank", name="vp")
+        def flip_e(i):
+            bank = psum.tile([P, L], BF16, tag="bank", name="e_flipped")
+            for j in range(TILES):
+                nc.tensor.transpose(bank[:, j * P:(j + 1) * P], e_rows[i][:, e_column(i, j):e_column(i, j) + P],
+                                    ident_bf16[:])
+            banks[("e", i)] = bank
+
+        def regroup_e(i):
+            tile = to_quantise.tile([P, L], BF16, tag="grouped", name="e_grouped", align_bytes=64)
+            nc.scalar.copy(out=tile[:].rearrange("p (g i t) -> p g i t", g=2, t=4),
+                           in_=banks[("e", i)][:].rearrange("p (g t i) -> p g i t", g=2, t=4))
+            grouped[("e", i)] = tile
+
+        def quantise_e(i):
+            quantise("e", i * 2 * P, 2 * P, grouped[("e", i)][:])
+
+        def v_bank(g, o):
+            bank = psum.tile([P, BANK], F32, tag="bank", name="v_bank")
             for t in range(4):
                 for c in range(2):
-                    mx(vp[:, t * P:(t + 1) * P], "x", c * L + (4 * g + t) * P, "w", c * L + o * P, P,
-                       c == 0, c == 1)
-            banks[("vp", g, o)] = vp
+                    mx_pass(bank[:, t * P:(t + 1) * P], "x", first_word("x", 4 * g + t, c), "w", first_word("w", o, c),
+                            P, c == 0, c == 1)
+            banks[("v", g, o)] = bank
 
-        def VBe(g, o):
-            oh, b = o // 4, o % 4
-            if ("v", g, oh) not in grps:
-                grps[("v", g, oh)] = gvp.tile([P, 2048], BF16, tag="gv", name="gv", align_bytes=64)
+        def v_regroup(g, o):
+            if o % 4 == 0:
+                grouped[("v", g, o // 4)] = v_to_quantise.tile([P, 4 * BANK], BF16, tag="v_grouped", name="v_grouped",
+                                                               align_bytes=64)
             nc.vector.tensor_tensor(
-                out=grps[("v", g, oh)][:, b * 512:(b + 1) * 512].rearrange("p (o t) -> p o t", t=4),
-                in0=banks[("vp", g, o)][:].rearrange("p (t o) -> p o t", t=4),
+                out=grouped[("v", g, o // 4)][:, (o % 4) * BANK:(o % 4 + 1) * BANK].rearrange("p (o t) -> p o t", t=4),
+                in0=banks[("v", g, o)][:].rearrange("p (t o) -> p o t", t=4),
                 in1=bias[:, o * P:(o + 1) * P].unsqueeze(2).to_broadcast([P, P, 4]),
                 op=ALU.add)
 
-        def QV(g, oh):
-            quant("v", g * L + oh * 512, 512, grps[("v", g, oh)][:])
+        def quantise_v(g, half):
+            quantise("v", g * L + half * BANK, BANK, grouped[("v", g, half)][:])
 
-        def OBp(i, oh):
-            op_ = psum.tile([P, 512], F32, tag="bank", name="op_")
+        def out_bank(i, half):
+            bank = psum.tile([P, BANK], F32, tag="bank", name="out_bank")
             for g in range(2):
-                mx(op_[:], "e", i * 256 + g * P, "v", g * L + oh * 512, 512, g == 0, g == 1)
-            banks[("o", i, oh)] = op_
+                mx_pass(bank[:], "e", i * 2 * P + g * P, "v", g * L + half * BANK, BANK, g == 0, g == 1)
+            banks[("out", i, half)] = bank
 
-        def OBe(i, oh, eng):
-            osb = outp.tile([P, 512], F32, tag="osb", name="osb")
-            if eng == "s":
-                nc.scalar.activation(out=osb[:], in_=banks[("o", i, oh)][:], func=ACT.Copy,
-                                     scale=rinv[:, i:i + 1])
+        def out_store(i, half, on_vector):
+            tile = stores.tile([P, BANK], F32, tag="result", name="result")
+            if on_vector:
+                nc.vector.tensor_scalar(out=tile[:], in0=banks[("out", i, half)][:],
+                                        scalar1=row_scale[:, i:i + 1], scalar2=None, op0=ALU.mult)
             else:
-                nc.vector.tensor_scalar(out=osb[:], in0=banks[("o", i, oh)][:],
-                                        scalar1=rinv[:, i:i + 1], scalar2=None, op0=ALU.mult)
-            nc.sync.dma_start(out=outv[:, i // 4, i % 4, oh * 512:(oh + 1) * 512], in_=osb[:])
+                nc.scalar.activation(out=tile[:], in_=banks[("out", i, half)][:], func=ACT.Copy,
+                                     scale=row_scale[:, i:i + 1])
+            nc.sync.dma_start(out=out_rows[:, i // 4, i % 4, half * BANK:(half + 1) * BANK], in_=tile[:])
 
-        def row_sums():
-            nc.vector.tensor_reduce(out=rsum[:], in_=sums[:].rearrange("p (i c) -> p i c", c=4)[:, :, 0:3],
-                                    axis=AX.X, op=ALU.add)
-            nc.vector.reciprocal(out=rinv[:], in_=rsum[:])
 
-        acts = {"T": T, "E": E, "Q": Q, "Bp": Bp, "Be": Be, "SCp": SCp, "SCv": SCv, "SCs": SCs, "TEp": TEp, "TEe": TEe,
-                "QE": QE, "VBp": VBp, "VBe": VBe, "QV": QV, "OBp": OBp, "OBe": OBe, "RS": row_sums}
-        for step in ORDER:
-            acts[step[0]](*step[1:])
+        head = [("k", n) for n in range(TILES)] + [("q", n) for n in range(4)]
+        for idx in range(len(head)):
+            flip(head[idx][0], head[idx][1])
+            regroup(head[idx][0], head[idx][1])
+            if idx == 3:
+                spread_bias()
+            if idx > 0:
+                quantise_input(head[idx - 1][0], head[idx - 1][1])
+        quantise_input(head[-1][0], head[-1][1])
+
+        more = ([("q", n) for n in range(4, TILES)] + [("x", n) for n in range(4)] + [("w", n) for n in range(4)]
+                + [("x", n) for n in range(4, TILES)])
+        copied = []
+        for i in range(TILES):
+            scores(i)
+            now = more[2 * i:2 * i + 2]
+            for name, n in now:
+                flip(name, n)
+            row_max(i)
+            for name, n in now:
+                regroup(name, n)
+            for name, n in copied:
+                quantise_input(name, n)
+            copied = now
+            exponentials(i)
+        for name, n in copied:
+            quantise_input(name, n)
+
+        e_copied = []
+        e_quantised = 0
+        for quarter in range(4):
+            g, half = quarter % 2, quarter // 2
+            if quarter == 1:
+                for n in range(4, TILES):
+                    flip("w", n)
+            for i in E_TILES_BEFORE_QUARTER[quarter]:
+                flip_e(i)
+            if quarter > 0:
+                quantise_v((quarter - 1) % 2, (quarter - 1) // 2)
+            if quarter == 1:
+                for n in range(4, TILES):
+                    regroup("w", n)
+                    if n > 4:
+                        quantise_input("w", n - 1)
+                quantise_input("w", TILES - 1)
+            for i in E_TILES_BEFORE_QUARTER[quarter]:
+                regroup_e(i)
+                e_copied.append(i)
+            for o in range(4 * half, 4 * half + 4):
+                v_bank(g, o)
+                v_regroup(g, o)
+                if o % 2 == 1 and e_quantised < len(e_copied):
+                    quantise_e(e_copied[e_quantised])
+                    e_quantised += 1
+            if quarter == 0:
+                row_scales()
+
+        for half in range(2):
+            for i in range(TILES):
+                out_bank(i, half)
+                if half == 0 and i == 0:
+                    quantise_v(1, 1)
+                if e_quantised < len(e_copied):
+                    quantise_e(e_copied[e_quantised])
+                    e_quantised += 1
+                out_store(i, half, i % OUT_BANKS_PER_VECTOR_TURN == OUT_BANKS_PER_VECTOR_TURN - 1)

@@ -24,6 +24,7 @@ LOADS = (("k", 0, 1), ("k", 1, 1), ("k", 2, 2), ("k", 4, 2), ("k", 6, 2), ("q", 
          ("x", 0, 4), ("w", 0, 4), ("x", 4, 4), ("w", 4, 4))
 E_TILES_BEFORE_QUARTER = ((), (0, 1, 2), (3, 4, 5), (6, 7))
 OUT_BANKS_PER_VECTOR_TURN = 4
+VECTOR_RESTS_IN_STEP = 1
 
 
 def e_column(i, j):
@@ -118,10 +119,14 @@ def tile_scaleddotproductattention_pa_kernel(tc, q, k, x, Wv, bv, out):
                                     pairs[:, n * BANK + cu * P:n * BANK + (cu + 1) * P], ident_f32[:])
             banks[(name, n)] = bank
 
-        def regroup(name, n):
+        def regroup(name, n, on_vector=False):
             tile = to_quantise.tile([P, L], BF16, tag="grouped", name="grouped", align_bytes=64)
-            nc.scalar.copy(out=tile[:].bitcast(F32).rearrange("p (c r u) -> p c r u", c=2, u=2),
-                           in_=banks[(name, n)][:].rearrange("p (c u r) -> p c r u", c=2, u=2))
+            side_by_side = tile[:].bitcast(F32).rearrange("p (c r u) -> p c r u", c=2, u=2)
+            flipped = banks[(name, n)][:].rearrange("p (c u r) -> p c r u", c=2, u=2)
+            if on_vector:
+                nc.vector.tensor_copy(out=side_by_side, in_=flipped)
+            else:
+                nc.scalar.copy(out=side_by_side, in_=flipped)
             grouped[(name, n)] = tile
 
         def quantise_input(name, n):
@@ -251,10 +256,14 @@ def tile_scaleddotproductattention_pa_kernel(tc, q, k, x, Wv, bv, out):
             for name, n in now:
                 flip(name, n)
             row_max(i)
-            for name, n in now:
-                regroup(name, n)
+            vector_helps = i % 3 != VECTOR_RESTS_IN_STEP
+            regroup(now[0][0], now[0][1])
+            if not vector_helps:
+                regroup(now[1][0], now[1][1])
             for name, n in copied:
                 quantise_input(name, n)
+            if vector_helps:
+                regroup(now[1][0], now[1][1], on_vector=True)
             copied = now
             exponentials(i)
         for name, n in copied:

@@ -22,6 +22,7 @@ MASKED = -3.4028234663852886e38
 
 LOADS = (("k", 0, 1), ("k", 1, 1), ("k", 2, 2), ("k", 4, 2), ("k", 6, 2), ("q", 0, 2), ("q", 2, 2), ("q", 4, 4),
          ("x", 0, 4), ("w", 0, 4), ("x", 4, 4), ("w", 4, 4))
+LOADS_BEFORE_BIAS = 2
 E_TILES_BEFORE_QUARTER = ((), (0, 1, 2), (3, 4, 5), (6, 7))
 OUT_BANKS_PER_VECTOR_TURN = 4
 VECTOR_RESTS_IN_STEP = 1
@@ -60,7 +61,6 @@ def tile_scaleddotproductattention_pa_kernel(tc, q, k, x, Wv, bv, out):
         row_scale = const.tile([P, TILES], F32, name="row_scale")
 
         nc.vector.memset(bias_row[:], 0.0)
-        nc.scalar.dma_start(out=bias_row[0:1, :], in_=bv.rearrange("(o n) -> o n", o=1))
         nc.vector.memset(ones[:], 1.0)
         make_identity(nc, ident_f32[:])
         make_identity(nc, ident_bf16[:])
@@ -82,7 +82,9 @@ def tile_scaleddotproductattention_pa_kernel(tc, q, k, x, Wv, bv, out):
         dram = {"w": Wv.rearrange("(n p) h -> p n h", p=P)}
         for name, src in (("k", k), ("q", q), ("x", x)):
             dram[name] = src.flatten_outer_dims().rearrange("(g p t) h -> p g t h", g=2, p=P, t=4)
-        for name, n0, count in LOADS:
+        for idx, (name, n0, count) in enumerate(LOADS):
+            if idx == LOADS_BEFORE_BIAS:
+                nc.sync.dma_start(out=bias_row[0:1, :], in_=bv.rearrange("(o n) -> o n", o=1))
             if name == "w":
                 rows = dram[name][:, n0:n0 + count, :]
             else:
@@ -159,18 +161,19 @@ def tile_scaleddotproductattention_pa_kernel(tc, q, k, x, Wv, bv, out):
 
         def row_max(i):
             diag = small.tile([P, P + 2], F32, tag="diag", name="diag")
-            top = small.tile([P, 1], F32, tag="top", name="top")
+            scaled = small.tile([P, P + 2], F32, tag="scaled", name="scaled")
+            shift = small.tile([P, 1], F32, tag="shift", name="shift")
             own, other = banks[("own", i)], banks[("other", i)]
             nc.vector.tensor_tensor(out=diag[:, 0:P], in0=own[:, 3 * P:BANK], in1=diag_mask[:], op=ALU.min)
             nc.vector.tensor_reduce(out=diag[:, P + 1:P + 2], in_=own[:, 0:3 * P], axis=AX.X, op=ALU.max)
             nc.vector.tensor_reduce(out=diag[:, P:P + 1], in_=other[:], axis=AX.X, op=ALU.max)
-            nc.vector.tensor_reduce(out=top[:], in_=diag[:], axis=AX.X, op=ALU.max)
+            nc.vector.tensor_scalar(out=scaled[:], in0=diag[:], scalar1=-1.0 / L, scalar2=None, op0=ALU.mult,
+                                    op1=ALU.min, accum_out=shift[:])
             grouped[("diag", i)] = diag
-            grouped[("top", i)] = top
+            grouped[("shift", i)] = shift
 
         def exponentials(i):
-            shift = small.tile([P, 1], F32, tag="shift", name="shift")
-            nc.scalar.mul(out=shift[:], in_=grouped[("top", i)][:], mul=-1.0 / L)
+            shift = grouped[("shift", i)]
             for part, column, n, src in ((0, 0, BANK, banks[("other", i)][:]),
                                          (1, BANK, 3 * P, banks[("own", i)][:, 0:3 * P]),
                                          (2, BANK + 3 * P, P, grouped[("diag", i)][:, 0:P])):
@@ -241,7 +244,7 @@ def tile_scaleddotproductattention_pa_kernel(tc, q, k, x, Wv, bv, out):
         for idx in range(len(head)):
             flip(head[idx][0], head[idx][1])
             regroup(head[idx][0], head[idx][1])
-            if idx == 3:
+            if idx == LOADS_BEFORE_BIAS - 1:
                 spread_bias()
             if idx > 0:
                 quantise_input(head[idx - 1][0], head[idx - 1][1])

@@ -22,7 +22,8 @@ MASKED = -3.4028234663852886e38
 
 LOADS = (("k", 0, 1), ("k", 1, 1), ("k", 2, 2), ("k", 4, 2), ("k", 6, 2), ("q", 0, 2), ("q", 2, 2), ("q", 4, 4),
          ("x", 0, 4), ("w", 0, 4), ("x", 4, 4), ("w", 4, 4))
-LOADS_BEFORE_BIAS = 2
+LOADS_BEFORE_BIAS = 5
+TILES_BEFORE_BIAS = 10
 E_TILES_BEFORE_QUARTER = ((), (0, 1, 2), (3, 4, 5), (6, 7))
 OUT_BANKS_PER_VECTOR_TURN = 4
 VECTOR_RESTS_IN_STEP = 1
@@ -244,7 +245,7 @@ def tile_scaleddotproductattention_pa_kernel(tc, q, k, x, Wv, bv, out):
         for idx in range(len(head)):
             flip(head[idx][0], head[idx][1])
             regroup(head[idx][0], head[idx][1])
-            if idx == LOADS_BEFORE_BIAS - 1:
+            if idx == TILES_BEFORE_BIAS - 1:
                 spread_bias()
             if idx > 0:
                 quantise_input(head[idx - 1][0], head[idx - 1][1])

@@ -20,23 +20,21 @@ TILES = L // P
 BANK = 512
 MASKED = -3.4028234663852886e38
 
-LOADS = (("k", 0, 1), ("k", 1, 1), ("k", 2, 2), ("k", 4, 2), ("k", 6, 2), ("q", 0, 2), ("q", 2, 2), ("q", 4, 4),
-         ("x", 0, 4), ("w", 0, 4), ("x", 4, 4), ("w", 4, 4))
-LOADS_BEFORE_BIAS = 5
-TILES_BEFORE_BIAS = 10
-E_TILES_BEFORE_QUARTER = ((), (0, 1, 2), (3, 4, 5), (6, 7))
-OUT_BANKS_PER_VECTOR_TURN = 4
-VECTOR_RESTS_IN_STEP = 1
+LOADS = (("x", 0, 1), ("x", 1, 1), ("x", 2, 2), ("w", 0, 2), ("w", 2, 2), ("x", 4, 2), ("x", 6, 2), ("k", 0, 4),
+         ("k", 4, 4), ("q", 0, 4), ("w", 4, 4), ("q", 4, 4))
+LOADS_BEFORE_BIAS = 4
 
 
-def e_column(i, j):
-    if j // 4 != i // 4:
-        return (j % 4) * P
-    if (j % 4) // 2 != (i % 4) // 2:
-        return BANK + (j % 2) * P
-    if j != i:
-        return BANK + 2 * P
-    return BANK + 3 * P
+WARM = (5, 1, 1, 1, 1, 1, 1, 2)
+PLAN = (
+    ("x", (0,), "long", ()), ("x", (1,), "long", ()), ("s", 1), ("x", (2,), "long", ()), ("s", 1), ("x", (3,), "long", ()), ("s", 1),
+    ("w", (0,), "long", ()), ("s", 1), ("w", (1,), "long", ()), ("b",), ("s", 2),
+    ("w", (2, 3), "long", ()), ("x", (4, 5), "long", ()),
+    ("v", 0, 0, 0, 1), ("v", 0, 1, 0, 2), ("x", (6, 7), "long", ()), ("k", (0, 1), "long", ()), ("s", 1),
+    ("v", 0, 2, 0, 2), ("v", 0, 3, 0, 1), ("k", (2, 3, 4, 5), "long", ()), ("s", 2),
+    ("v", 1, 0, 0, 2), ("v", 1, 1, 0, 1), ("q", (0,), "long", ()), ("k", (6, 7), "long", ()), ("q", (1,), "long", ()), ("s", 1),
+    ("v", 1, 2, 2, 2), ("v", 1, 3, 1, 3),
+)
 
 
 def tile_scaleddotproductattention_pa_kernel(tc, q, k, x, Wv, bv, out):
@@ -44,31 +42,35 @@ def tile_scaleddotproductattention_pa_kernel(tc, q, k, x, Wv, bv, out):
     with ExitStack() as ctx:
         const = ctx.enter_context(tc.tile_pool(name="const", bufs=1))
         keep = ctx.enter_context(tc.tile_pool(name="keep", bufs=1))
-        to_quantise = ctx.enter_context(tc.tile_pool(name="to_quantise", bufs=6))
+        to_quantise = ctx.enter_context(tc.tile_pool(name="to_quantise", bufs=10))
         v_to_quantise = ctx.enter_context(tc.tile_pool(name="v_to_quantise", bufs=2))
         small = ctx.enter_context(tc.tile_pool(name="small", bufs=3))
         stores = ctx.enter_context(tc.tile_pool(name="stores", bufs=12))
-        psum = ctx.enter_context(tc.psum_pool(name="psum", bufs=8))
+        psum = ctx.enter_context(tc.psum_pool(name="psum", bufs=4))
         ctx.enter_context(tc.manual_schedule())
 
         ident_f32 = const.tile([P, P], F32, name="ident_f32")
-        ident_bf16 = const.tile([P, P], BF16, name="ident_bf16")
         diag_mask = const.tile([P, P], F32, name="diag_mask")
+        pair_mask = [const.tile([P, 2 * P], F32, name="pair_mask%d" % a) for a in range(2)]
         ones = const.tile([P, P], BF16, name="ones")
+        warm_rows = const.tile([P, BANK], BF16, name="warm_rows")
         bias_row = const.tile([P, L], BF16, name="bias_row")
         bias = const.tile([P, L], F32, name="bias")
         part_sums = const.tile([P, 4 * TILES], F32, name="part_sums")
         row_sum = const.tile([P, TILES], F32, name="row_sum")
         row_scale = const.tile([P, TILES], F32, name="row_scale")
 
-        nc.vector.memset(bias_row[:], 0.0)
         nc.vector.memset(ones[:], 1.0)
+        nc.vector.memset(warm_rows[:], 1.0)
+        nc.vector.memset(bias_row[:], 0.0)
         make_identity(nc, ident_f32[:])
-        make_identity(nc, ident_bf16[:])
         nc.vector.tensor_scalar(out=diag_mask[:], in0=ident_f32[:], scalar1=-2.0, scalar2=1.0,
                                 op0=ALU.mult, op1=ALU.add)
         nc.vector.tensor_scalar(out=diag_mask[:], in0=diag_mask[:], scalar1=-MASKED, scalar2=0.0,
                                 op0=ALU.mult, op1=ALU.add)
+        for a in range(2):
+            nc.vector.memset(pair_mask[a][:], -MASKED)
+            nc.vector.tensor_copy(out=pair_mask[a][:].rearrange("p (r a) -> p a r", a=2)[:, a, :], in_=diag_mask[:])
 
         raw = {}
         words = {}
@@ -114,8 +116,8 @@ def tile_scaleddotproductattention_pa_kernel(tc, q, k, x, Wv, bv, out):
         banks = {}
         grouped = {}
 
-        def flip(name, n):
-            bank = psum.tile([P, BANK], F32, tag="bank", name="flipped")
+        def flip(name, n, ring="short"):
+            bank = psum.tile([P, BANK], F32, tag=ring, name="flipped")
             pairs = raw[name][:].bitcast(F32)
             for cu in range(4):
                 nc.tensor.transpose(bank[:, cu * P:(cu + 1) * P],
@@ -140,71 +142,83 @@ def tile_scaleddotproductattention_pa_kernel(tc, q, k, x, Wv, bv, out):
             else:
                 quantise(name, first_word(name, n, 0), 2 * P, tile[:])
 
+        warm_bank = psum.tile([P, BANK], F32, tag="short", name="warm_bank")
+
+        def keep_warm(count):
+            for z in range(count):
+                nc.tensor.matmul(warm_bank[:], lhsT=ones[:], rhs=warm_rows[:], start=True, stop=True)
+
         def spread_bias():
             for half in range(2):
-                bank = psum.tile([P, BANK], F32, tag="bank", name="bias_bank")
+                bank = psum.tile([P, BANK], F32, tag="short", name="bias_bank")
                 nc.tensor.matmul(bank[:], lhsT=ones[:], rhs=bias_row[:, half * BANK:(half + 1) * BANK],
                                  start=True, stop=True)
                 nc.vector.tensor_copy(out=bias[:, half * BANK:(half + 1) * BANK], in_=bank[:])
 
         def scores(i):
-            half, pair = i // 4, (i % 4) // 2
-            own = psum.tile([P, BANK], F32, tag="bank", name="own_half")
-            other = psum.tile([P, BANK], F32, tag="bank", name="other_half")
-            for bank, column, key_tile, n in ((own, 3 * P, i, P), (own, 2 * P, i ^ 1, P),
-                                              (own, 0, 4 * half + 2 * (1 - pair), 2 * P),
-                                              (other, 0, 4 * (1 - half), BANK)):
+            for place, half in (("own", i // 4), ("other", 1 - i // 4)):
+                bank = psum.tile([P, BANK], F32, tag="long", name="scores")
                 for c in range(2):
-                    mx_pass(bank[:, column:column + n], "q", first_word("q", i, c), "k", first_word("k", key_tile, c),
-                            n, c == 0, c == 1)
-            banks[("own", i)] = own
-            banks[("other", i)] = other
+                    mx_pass(bank[:], "q", first_word("q", i, c), "k", first_word("k", 4 * half, c), BANK,
+                            c == 0, c == 1)
+                banks[(place, i)] = bank
 
         def row_max(i):
-            diag = small.tile([P, P + 2], F32, tag="diag", name="diag")
-            scaled = small.tile([P, P + 2], F32, tag="scaled", name="scaled")
+            diag = small.tile([P, 2 * P + 2], F32, tag="diag", name="diag")
+            scaled = small.tile([P, 2 * P + 2], F32, tag="scaled", name="scaled")
             shift = small.tile([P, 1], F32, tag="shift", name="shift")
             own, other = banks[("own", i)], banks[("other", i)]
-            nc.vector.tensor_tensor(out=diag[:, 0:P], in0=own[:, 3 * P:BANK], in1=diag_mask[:], op=ALU.min)
-            nc.vector.tensor_reduce(out=diag[:, P + 1:P + 2], in_=own[:, 0:3 * P], axis=AX.X, op=ALU.max)
-            nc.vector.tensor_reduce(out=diag[:, P:P + 1], in_=other[:], axis=AX.X, op=ALU.max)
+            pair = (i % 4) // 2
+            nc.vector.tensor_tensor(out=diag[:, 0:2 * P].rearrange("p (r a) -> p r a", a=2),
+                                    in0=own[:, 2 * P * pair:2 * P * (pair + 1)].rearrange("p (a r) -> p r a", a=2),
+                                    in1=pair_mask[i % 2][:].rearrange("p (r a) -> p r a", a=2), op=ALU.min)
+            nc.vector.tensor_reduce(out=diag[:, 2 * P + 1:2 * P + 2], in_=own[:, 2 * P * (1 - pair):2 * P * (2 - pair)],
+                                    axis=AX.X, op=ALU.max)
+            nc.vector.tensor_reduce(out=diag[:, 2 * P:2 * P + 1], in_=other[:], axis=AX.X, op=ALU.max)
+            settle(1)
             nc.vector.tensor_scalar(out=scaled[:], in0=diag[:], scalar1=-1.0 / L, scalar2=None, op0=ALU.mult,
                                     op1=ALU.min, accum_out=shift[:])
             grouped[("diag", i)] = diag
             grouped[("shift", i)] = shift
 
         def exponentials(i):
-            shift = grouped[("shift", i)]
-            for part, column, n, src in ((0, 0, BANK, banks[("other", i)][:]),
-                                         (1, BANK, 3 * P, banks[("own", i)][:, 0:3 * P]),
-                                         (2, BANK + 3 * P, P, grouped[("diag", i)][:, 0:P])):
-                nc.scalar.activation(out=e_rows[i][:, column:column + n], in_=src, func=ACT.Exp,
-                                     bias=shift[:], scale=1.0 / L,
-                                     accum_out=part_sums[:, 4 * i + part:4 * i + part + 1])
+            half, pair = i // 4, (i % 4) // 2
+            row = e_rows[i]
+            for part, first, pairs, src in (
+                    (0, 2 * (1 - half), 2, banks[("other", i)][:]),
+                    (1, 2 * half + 1 - pair, 1, banks[("own", i)][:, 2 * P * (1 - pair):2 * P * (2 - pair)]),
+                    (2, 2 * half + pair, 1, grouped[("diag", i)][:, 0:2 * P])):
+                order = "p (u r a) -> p u r a" if part == 2 else "p (u a r) -> p u r a"
+                nc.scalar.activation(
+                    out=row[:, 2 * P * first:2 * P * (first + pairs)].rearrange("p (u r a) -> p u r a", u=pairs, a=2),
+                    in_=src.rearrange(order, u=pairs, a=2), func=ACT.Exp, bias=grouped[("shift", i)][:],
+                    scale=1.0 / L, accum_out=part_sums[:, 4 * i + part:4 * i + part + 1])
 
-        def row_scales():
-            nc.vector.tensor_reduce(out=row_sum[:], in_=part_sums[:].rearrange("p (i m) -> p i m", m=4)[:, :, 0:3],
+        def row_scales(first, count):
+            part = slice(first, first + count)
+            nc.vector.tensor_reduce(out=row_sum[:, first:first + count],
+                                    in_=part_sums[:, 4 * first:4 * (first + count)].rearrange("p (i m) -> p i m", m=4)[:, :, 0:3],
                                     axis=AX.X, op=ALU.add)
-            nc.vector.reciprocal(out=row_scale[:], in_=row_sum[:])
+            nc.vector.reciprocal(out=row_scale[:, first:first + count], in_=row_sum[:, first:first + count])
 
         def flip_e(i):
-            bank = psum.tile([P, L], BF16, tag="bank", name="e_flipped")
-            for j in range(TILES):
-                nc.tensor.transpose(bank[:, j * P:(j + 1) * P], e_rows[i][:, e_column(i, j):e_column(i, j) + P],
-                                    ident_bf16[:])
+            bank = psum.tile([P, BANK], F32, tag="short", name="e_flipped")
+            pairs = e_rows[i][:].bitcast(F32)
+            for gu in range(4):
+                nc.tensor.transpose(bank[:, gu * P:(gu + 1) * P], pairs[:, gu * P:(gu + 1) * P], ident_f32[:])
             banks[("e", i)] = bank
 
         def regroup_e(i):
             tile = to_quantise.tile([P, L], BF16, tag="grouped", name="e_grouped", align_bytes=64)
-            nc.scalar.copy(out=tile[:].rearrange("p (g i t) -> p g i t", g=2, t=4),
-                           in_=banks[("e", i)][:].rearrange("p (g t i) -> p g i t", g=2, t=4))
+            nc.scalar.copy(out=tile[:].bitcast(F32).rearrange("p (g i u) -> p g i u", g=2, u=2),
+                           in_=banks[("e", i)][:].rearrange("p (g u i) -> p g i u", g=2, u=2))
             grouped[("e", i)] = tile
 
         def quantise_e(i):
             quantise("e", i * 2 * P, 2 * P, grouped[("e", i)][:])
 
         def v_bank(g, o):
-            bank = psum.tile([P, BANK], F32, tag="bank", name="v_bank")
+            bank = psum.tile([P, BANK], F32, tag="short", name="v_bank")
             for t in range(4):
                 for c in range(2):
                     mx_pass(bank[:, t * P:(t + 1) * P], "x", first_word("x", 4 * g + t, c), "w", first_word("w", o, c),
@@ -225,7 +239,7 @@ def tile_scaleddotproductattention_pa_kernel(tc, q, k, x, Wv, bv, out):
             quantise("v", g * L + half * BANK, BANK, grouped[("v", g, half)][:])
 
         def out_bank(i, half):
-            bank = psum.tile([P, BANK], F32, tag="bank", name="out_bank")
+            bank = psum.tile([P, BANK], F32, tag="short", name="out_bank")
             for g in range(2):
                 mx_pass(bank[:], "e", i * 2 * P + g * P, "v", g * L + half * BANK, BANK, g == 0, g == 1)
             banks[("out", i, half)] = bank
@@ -240,74 +254,99 @@ def tile_scaleddotproductattention_pa_kernel(tc, q, k, x, Wv, bv, out):
                                      scale=row_scale[:, i:i + 1])
             nc.sync.dma_start(out=out_rows[:, i // 4, i % 4, half * BANK:(half + 1) * BANK], in_=tile[:])
 
+        waiting = []
 
-        head = [("k", n) for n in range(TILES)] + [("q", n) for n in range(4)]
-        for idx in range(len(head)):
-            flip(head[idx][0], head[idx][1])
-            regroup(head[idx][0], head[idx][1])
-            if idx == TILES_BEFORE_BIAS - 1:
+        settled = [0]
+
+        def settle(count):
+            for z in range(min(count, len(waiting) - settled[0])):
+                waiting[settled[0]]()
+                settled[0] += 1
+
+        def bring(tiles, ring, vector=()):
+            for name, n in tiles:
+                flip(name, n, ring)
+            for name, n in tiles:
+                regroup(name, n, on_vector=(name, n) in vector)
+                waiting.append(lambda name=name, n=n: quantise_input(name, n))
+
+        def values(g, o, count=1):
+            v_bank(g, o)
+            v_regroup(g, o)
+            settle(count)
+            if o % 4 == 3:
+                waiting.append(lambda: quantise_v(g, o // 4))
+
+        plan = PLAN
+        keep_warm(WARM[0])
+        count = 0
+        for piece in plan:
+            if piece[0] in ("x", "w", "k", "q"):
+                count += 1
+            if piece[0] == "v":
+                settle(piece[3])
+                values(piece[1], piece[2], piece[4])
+            elif piece[0] == "b":
                 spread_bias()
-            if idx > 0:
-                quantise_input(head[idx - 1][0], head[idx - 1][1])
-        quantise_input(head[-1][0], head[-1][1])
-
-        more = ([("q", n) for n in range(4, TILES)] + [("x", n) for n in range(4)] + [("w", n) for n in range(4)]
-                + [("x", n) for n in range(4, TILES)])
-        copied = []
-        for i in range(TILES):
-            scores(i)
-            now = more[2 * i:2 * i + 2]
-            for name, n in now:
+            elif piece[0] == "s":
+                settle(piece[1])
+            else:
+                bring([(piece[0], n) for n in piece[1]], piece[2], [(piece[0], n) for n in piece[3]])
+                if count < len(WARM):
+                    keep_warm(WARM[count])
+        for s in range(TILES + 1):
+            settle(len(waiting) - settled[0] - (1 if s < TILES else 0))
+            if s < TILES:
+                scores(s)
+            if 1 <= s:
+                v_bank((s - 1) // 4, 4 + (s - 1) % 4)
+            if 4 <= s:
+                out_bank(s - 4, 0)
+            fl = []
+            if 2 <= s:
+                flip_e(s - 2)
+            if s + 2 < TILES:
+                fl.append(("q", s + 2))
+            if s < 2:
+                fl.append(("w", 4 + 2 * s))
+                fl.append(("w", 5 + 2 * s))
+            for name, n in fl:
                 flip(name, n)
-            row_max(i)
-            vector_helps = i % 3 != VECTOR_RESTS_IN_STEP
-            regroup(now[0][0], now[0][1])
-            if not vector_helps:
-                regroup(now[1][0], now[1][1])
-            for name, n in copied:
-                quantise_input(name, n)
-            if vector_helps:
-                regroup(now[1][0], now[1][1], on_vector=True)
-            copied = now
-            exponentials(i)
-        for name, n in copied:
-            quantise_input(name, n)
-
-        e_copied = []
-        e_quantised = 0
-        for quarter in range(4):
-            g, half = quarter % 2, quarter // 2
-            if quarter == 1:
-                for n in range(4, TILES):
-                    flip("w", n)
-            for i in E_TILES_BEFORE_QUARTER[quarter]:
-                flip_e(i)
-            if quarter > 0:
-                quantise_v((quarter - 1) % 2, (quarter - 1) // 2)
-            if quarter == 1:
-                for n in range(4, TILES):
-                    regroup("w", n)
-                    if n > 4:
-                        quantise_input("w", n - 1)
-                quantise_input("w", TILES - 1)
-            for i in E_TILES_BEFORE_QUARTER[quarter]:
-                regroup_e(i)
-                e_copied.append(i)
-            for o in range(4 * half, 4 * half + 4):
-                v_bank(g, o)
-                v_regroup(g, o)
-                if o % 2 == 1 and e_quantised < len(e_copied):
-                    quantise_e(e_copied[e_quantised])
-                    e_quantised += 1
-            if quarter == 0:
-                row_scales()
-
-        for half in range(2):
-            for i in range(TILES):
-                out_bank(i, half)
-                if half == 0 and i == 0:
-                    quantise_v(1, 1)
-                if e_quantised < len(e_copied):
-                    quantise_e(e_copied[e_quantised])
-                    e_quantised += 1
-                out_store(i, half, i % OUT_BANKS_PER_VECTOR_TURN == OUT_BANKS_PER_VECTOR_TURN - 1)
+            if 1 <= s <= TILES:
+                exponentials(s - 1)
+            if s < TILES:
+                row_max(s)
+            if 2 <= s:
+                regroup_e(s - 2)
+            for name, n in fl:
+                regroup(name, n)
+            if 4 <= s:
+                out_store(s - 4, 0, False)
+            if 1 <= s:
+                v_regroup((s - 1) // 4, 4 + (s - 1) % 4)
+            if s in (3, 5, 7, 8):
+                row_scales({3: 0, 5: 2, 7: 4, 8: 6}[s], 2)
+            for name, n in fl:
+                waiting.append(lambda name=name, n=n: quantise_input(name, n))
+            if s == 8:
+                waiting.append(lambda: quantise_v(1, 1))
+            if 2 <= s:
+                waiting.append(lambda s=s: quantise_e(s - 2))
+            if s == 4:
+                waiting.append(lambda: quantise_v(0, 1))
+        def finish(i, half, v):
+            out_bank(i, half)
+            out_store(i, half, v)
+        settle(9)
+        finish(5, 0, False)
+        flip_e(7)
+        finish(0, 1, True)
+        regroup_e(7)
+        finish(1, 1, True)
+        quantise_e(7)
+        finish(6, 0, False)
+        for i in range(2, 6):
+            finish(i, 1, i % 2 == 1)
+        finish(7, 0, False)
+        finish(6, 1, True)
+        finish(7, 1, False)

@@ -25,7 +25,7 @@ LOADS = (("x", 0, 1), ("x", 1, 1), ("x", 2, 2), ("w", 0, 2), ("w", 2, 2), ("x", 
 LOADS_BEFORE_BIAS = 4
 
 
-WARM = (5, 1, 1, 1, 1, 1, 1, 2)
+WARM = (4, 1, 1, 1, 1, 1, 1, 2)
 PLAN = (
     ("x", (0,), "long", ()), ("x", (1,), "long", ()), ("s", 1), ("x", (2,), "long", ()), ("s", 1), ("x", (3,), "long", ()), ("s", 1),
     ("w", (0,), "long", ()), ("s", 1), ("w", (1,), "long", ()), ("b",), ("s", 2),
@@ -316,12 +316,12 @@ def tile_scaleddotproductattention_pa_kernel(tc, q, k, x, Wv, bv, out):
                 exponentials(s - 1)
             if s < TILES:
                 row_max(s)
+            if 4 <= s:
+                out_store(s - 4, 0, False)
             if 2 <= s:
                 regroup_e(s - 2)
             for name, n in fl:
                 regroup(name, n)
-            if 4 <= s:
-                out_store(s - 4, 0, False)
             if 1 <= s:
                 v_regroup((s - 1) // 4, 4 + (s - 1) % 4)
             if s in (3, 5, 7, 8):

@@ -20,8 +20,8 @@ TILES = L // P
 BANK = 512
 MASKED = -3.4028234663852886e38
 
-LOADS = (("x", 0, 1), ("x", 1, 1), ("x", 2, 2), ("w", 0, 2), ("w", 2, 2), ("x", 4, 2), ("x", 6, 2), ("k", 0, 4),
-         ("k", 4, 4), ("q", 0, 4), ("w", 4, 4), ("q", 4, 4))
+LOADS = (("x", 0, 1), ("x", 1, 1), ("x", 2, 2), ("w", 0, 2), ("w", 2, 2), ("x", 4, 2), ("x", 6, 2), ("k", 0, 2), ("k", 2, 2),
+         ("k", 4, 2), ("q", 0, 2), ("k", 6, 2), ("w", 4, 2), ("q", 2, 2), ("w", 6, 2), ("q", 4, 4))
 LOADS_BEFORE_BIAS = 4
 
 
@@ -82,18 +82,14 @@ def tile_scaleddotproductattention_pa_kernel(tc, q, k, x, Wv, bv, out):
             scales[name] = keep.tile([P, 2 * L], U8, name="scales_" + name, align_bytes=64)
         e_rows = [keep.tile([P, L], BF16, name="e_rows%d" % i) for i in range(TILES)]
 
-        dram = {"w": Wv.rearrange("(n p) h -> p n h", p=P)}
+        dram = {"w": Wv.rearrange("(g p t) h -> p g t h", g=2, p=P, t=4)}
         for name, src in (("k", k), ("q", q), ("x", x)):
             dram[name] = src.flatten_outer_dims().rearrange("(g p t) h -> p g t h", g=2, p=P, t=4)
         for idx, (name, n0, count) in enumerate(LOADS):
             if idx == LOADS_BEFORE_BIAS:
                 nc.sync.dma_start(out=bias_row[0:1, :], in_=bv.rearrange("(o n) -> o n", o=1))
-            if name == "w":
-                rows = dram[name][:, n0:n0 + count, :]
-            else:
-                rows = dram[name][:, n0 // 4, n0 % 4:n0 % 4 + count, :]
             nc.sync.dma_start(out=raw[name][:, n0 * L:(n0 + count) * L].rearrange("p (n h) -> p n h", n=count),
-                              in_=rows)
+                              in_=dram[name][:, n0 // 4, n0 % 4:n0 % 4 + count, :])
         out_rows = out.flatten_outer_dims().rearrange("(g p t) o -> p g t o", g=2, p=P, t=4)
 
         def first_word(name, n, c):
@@ -153,7 +149,9 @@ def tile_scaleddotproductattention_pa_kernel(tc, q, k, x, Wv, bv, out):
                 bank = psum.tile([P, BANK], F32, tag="short", name="bias_bank")
                 nc.tensor.matmul(bank[:], lhsT=ones[:], rhs=bias_row[:, half * BANK:(half + 1) * BANK],
                                  start=True, stop=True)
-                nc.vector.tensor_copy(out=bias[:, half * BANK:(half + 1) * BANK], in_=bank[:])
+                nc.vector.tensor_copy(
+                    out=bias[:, half * BANK:(half + 1) * BANK].rearrange("p (t o) -> p t o", t=4),
+                    in_=bank[:].rearrange("p (o t) -> p t o", t=4))
 
         def scores(i):
             for place, half in (("own", i // 4), ("other", 1 - i // 4)):
@@ -246,12 +244,13 @@ def tile_scaleddotproductattention_pa_kernel(tc, q, k, x, Wv, bv, out):
 
         def out_store(i, half, on_vector):
             tile = stores.tile([P, BANK], F32, tag="result", name="result")
+            natural = tile[:].rearrange("p (o t) -> p o t", t=4)
+            by_tile = banks[("out", i, half)][:].rearrange("p (t o) -> p o t", t=4)
             if on_vector:
-                nc.vector.tensor_scalar(out=tile[:], in0=banks[("out", i, half)][:],
-                                        scalar1=row_scale[:, i:i + 1], scalar2=None, op0=ALU.mult)
+                nc.vector.tensor_scalar(out=natural, in0=by_tile, scalar1=row_scale[:, i:i + 1], scalar2=None,
+                                        op0=ALU.mult)
             else:
-                nc.scalar.activation(out=tile[:], in_=banks[("out", i, half)][:], func=ACT.Copy,
-                                     scale=row_scale[:, i:i + 1])
+                nc.scalar.activation(out=natural, in_=by_tile, func=ACT.Copy, scale=row_scale[:, i:i + 1])
             nc.sync.dma_start(out=out_rows[:, i // 4, i % 4, half * BANK:(half + 1) * BANK], in_=tile[:])
 
         waiting = []

@@ -22,13 +22,12 @@ MASKED = -3.4028234663852886e38
 
 LOADS = (("x", 0, 1), ("x", 1, 1), ("x", 2, 2), ("w", 0, 2), ("w", 2, 2), ("x", 4, 2), ("x", 6, 2), ("k", 0, 2), ("k", 2, 2),
          ("k", 4, 2), ("q", 0, 2), ("k", 6, 2), ("w", 4, 2), ("q", 2, 2), ("w", 6, 2), ("q", 4, 4))
-LOADS_BEFORE_BIAS = 4
 
 
-WARM = (4, 1, 1, 1, 1, 1, 1, 2)
+WARM = (4, 1, 1, 1, 1, 1, 1, 1)
 PLAN = (
-    ("x", (0,), "long", ()), ("x", (1,), "long", ()), ("s", 1), ("x", (2,), "long", ()), ("s", 1), ("x", (3,), "long", ()), ("s", 1),
-    ("w", (0,), "long", ()), ("s", 1), ("w", (1,), "long", ()), ("b",), ("s", 2),
+    ("x", (0,), "long", ()), ("x", (1,), "long", ()), ("s", 1), ("x", (2,), "long", ()), ("b",), ("s", 1), ("x", (3,), "long", ()), ("s", 1),
+    ("w", (0,), "long", ()), ("s", 1), ("w", (1,), "long", ()), ("s", 2),
     ("w", (2, 3), "long", ()), ("x", (4, 5), "long", ()),
     ("v", 0, 0, 0, 1), ("v", 0, 1, 0, 2), ("x", (6, 7), "long", ()), ("k", (0, 1), "long", ()), ("s", 1),
     ("v", 0, 2, 0, 2), ("v", 0, 3, 0, 1), ("k", (2, 3, 4, 5), "long", ()), ("s", 2),
@@ -60,9 +59,10 @@ def tile_scaleddotproductattention_pa_kernel(tc, q, k, x, Wv, bv, out):
         row_sum = const.tile([P, TILES], F32, name="row_sum")
         row_scale = const.tile([P, TILES], F32, name="row_scale")
 
+        nc.vector.memset(bias_row[:], 0.0)
+        nc.scalar.dma_start(out=bias_row[0:1, :], in_=bv.rearrange("(o n) -> o n", o=1))
         nc.vector.memset(ones[:], 1.0)
         nc.vector.memset(warm_rows[:], 1.0)
-        nc.vector.memset(bias_row[:], 0.0)
         make_identity(nc, ident_f32[:])
         nc.vector.tensor_scalar(out=diag_mask[:], in0=ident_f32[:], scalar1=-2.0, scalar2=1.0,
                                 op0=ALU.mult, op1=ALU.add)
@@ -85,9 +85,7 @@ def tile_scaleddotproductattention_pa_kernel(tc, q, k, x, Wv, bv, out):
         dram = {"w": Wv.rearrange("(g p t) h -> p g t h", g=2, p=P, t=4)}
         for name, src in (("k", k), ("q", q), ("x", x)):
             dram[name] = src.flatten_outer_dims().rearrange("(g p t) h -> p g t h", g=2, p=P, t=4)
-        for idx, (name, n0, count) in enumerate(LOADS):
-            if idx == LOADS_BEFORE_BIAS:
-                nc.sync.dma_start(out=bias_row[0:1, :], in_=bv.rearrange("(o n) -> o n", o=1))
+        for name, n0, count in LOADS:
             nc.sync.dma_start(out=raw[name][:, n0 * L:(n0 + count) * L].rearrange("p (n h) -> p n h", n=count),
                               in_=dram[name][:, n0 // 4, n0 % 4:n0 % 4 + count, :])
         out_rows = out.flatten_outer_dims().rearrange("(g p t) o -> p g t o", g=2, p=P, t=4)

@@ -20,20 +20,17 @@ TILES = L // P
 BANK = 512
 MASKED = -3.4028234663852886e38
 
-LOADS = (("x", 0, 1), ("x", 1, 1), ("x", 2, 2), ("w", 0, 2), ("w", 2, 2), ("x", 4, 2), ("x", 6, 2), ("k", 0, 2), ("k", 2, 2),
-         ("k", 4, 2), ("q", 0, 2), ("k", 6, 2), ("w", 4, 2), ("q", 2, 2), ("w", 6, 2), ("q", 4, 4))
+LOADS = (("x", 0, 1), ("x", 1, 1), ("x", 2, 1), ("x", 3, 1), ("w", 0, 1), ("w", 1, 1), ("w", 2, 2), ("x", 4, 2),
+         ("x", 6, 2), ("k", 0, 2), ("k", 2, 2), ("k", 4, 2), ("q", 0, 2), ("k", 6, 2), ("w", 4, 2), ("q", 2, 2),
+         ("w", 6, 2), ("q", 4, 4))
 
-
-WARM = (4, 1, 1, 1, 1, 1, 1, 1)
-PLAN = (
-    ("x", (0,), "long", ()), ("x", (1,), "long", ()), ("s", 1), ("x", (2,), "long", ()), ("b",), ("s", 1), ("x", (3,), "long", ()), ("s", 1),
-    ("w", (0,), "long", ()), ("s", 1), ("w", (1,), "long", ()), ("s", 2),
-    ("w", (2, 3), "long", ()), ("x", (4, 5), "long", ()),
-    ("v", 0, 0, 0, 1), ("v", 0, 1, 0, 2), ("x", (6, 7), "long", ()), ("k", (0, 1), "long", ()), ("s", 1),
-    ("v", 0, 2, 0, 2), ("v", 0, 3, 0, 1), ("k", (2, 3, 4, 5), "long", ()), ("s", 2),
-    ("v", 1, 0, 0, 2), ("v", 1, 1, 0, 1), ("q", (0,), "long", ()), ("k", (6, 7), "long", ()), ("q", (1,), "long", ()), ("s", 1),
-    ("v", 1, 2, 2, 2), ("v", 1, 3, 1, 3),
-)
+FIRST_TILES = (("x", 0), ("x", 1), ("x", 2), ("x", 3), ("w", 0), ("w", 1))
+GROUPS = (((("w", 2), ("w", 3), ("x", 4), ("x", 5)), ((0, 0), (0, 1))),
+          ((("x", 6), ("x", 7), ("k", 0), ("k", 1)), ((0, 2), (0, 3))),
+          ((("k", 2), ("k", 3), ("k", 4), ("k", 5)), ((1, 0), (1, 1))),
+          ((("q", 0), ("k", 6), ("k", 7), ("q", 1)), ((1, 2), (1, 3))))
+DUMMIES_AT_START = 4
+OUT_LAG = 4
 
 
 def tile_scaleddotproductattention_pa_kernel(tc, q, k, x, Wv, bv, out):
@@ -48,11 +45,11 @@ def tile_scaleddotproductattention_pa_kernel(tc, q, k, x, Wv, bv, out):
         psum = ctx.enter_context(tc.psum_pool(name="psum", bufs=4))
         ctx.enter_context(tc.manual_schedule())
 
-        ident_f32 = const.tile([P, P], F32, name="ident_f32")
+        ident = const.tile([P, P], F32, name="ident")
         diag_mask = const.tile([P, P], F32, name="diag_mask")
         pair_mask = [const.tile([P, 2 * P], F32, name="pair_mask%d" % a) for a in range(2)]
         ones = const.tile([P, P], BF16, name="ones")
-        warm_rows = const.tile([P, BANK], BF16, name="warm_rows")
+        dummy_rows = const.tile([P, BANK], BF16, name="dummy_rows")
         bias_row = const.tile([P, L], BF16, name="bias_row")
         bias = const.tile([P, L], F32, name="bias")
         part_sums = const.tile([P, 4 * TILES], F32, name="part_sums")
@@ -62,9 +59,9 @@ def tile_scaleddotproductattention_pa_kernel(tc, q, k, x, Wv, bv, out):
         nc.vector.memset(bias_row[:], 0.0)
         nc.scalar.dma_start(out=bias_row[0:1, :], in_=bv.rearrange("(o n) -> o n", o=1))
         nc.vector.memset(ones[:], 1.0)
-        nc.vector.memset(warm_rows[:], 1.0)
-        make_identity(nc, ident_f32[:])
-        nc.vector.tensor_scalar(out=diag_mask[:], in0=ident_f32[:], scalar1=-2.0, scalar2=1.0,
+        nc.vector.memset(dummy_rows[:], 1.0)
+        make_identity(nc, ident[:])
+        nc.vector.tensor_scalar(out=diag_mask[:], in0=ident[:], scalar1=-2.0, scalar2=1.0,
                                 op0=ALU.mult, op1=ALU.add)
         nc.vector.tensor_scalar(out=diag_mask[:], in0=diag_mask[:], scalar1=-MASKED, scalar2=0.0,
                                 op0=ALU.mult, op1=ALU.add)
@@ -109,26 +106,27 @@ def tile_scaleddotproductattention_pa_kernel(tc, q, k, x, Wv, bv, out):
 
         banks = {}
         grouped = {}
+        waiting = []
 
-        def flip(name, n, ring="short"):
+        def settle(count):
+            for function, arguments in waiting[:count]:
+                function(*arguments)
+            waiting[:count] = []
+
+        def flip(name, n, ring):
             bank = psum.tile([P, BANK], F32, tag=ring, name="flipped")
-            pairs = raw[name][:].bitcast(F32)
+            pairs = e_rows[n][:].bitcast(F32) if name == "e" else raw[name][:, n * L:(n + 1) * L].bitcast(F32)
             for cu in range(4):
-                nc.tensor.transpose(bank[:, cu * P:(cu + 1) * P],
-                                    pairs[:, n * BANK + cu * P:n * BANK + (cu + 1) * P], ident_f32[:])
+                nc.tensor.transpose(bank[:, cu * P:(cu + 1) * P], pairs[:, cu * P:(cu + 1) * P], ident[:])
             banks[(name, n)] = bank
 
-        def regroup(name, n, on_vector=False):
+        def regroup(name, n):
             tile = to_quantise.tile([P, L], BF16, tag="grouped", name="grouped", align_bytes=64)
-            side_by_side = tile[:].bitcast(F32).rearrange("p (c r u) -> p c r u", c=2, u=2)
-            flipped = banks[(name, n)][:].rearrange("p (c u r) -> p c r u", c=2, u=2)
-            if on_vector:
-                nc.vector.tensor_copy(out=side_by_side, in_=flipped)
-            else:
-                nc.scalar.copy(out=side_by_side, in_=flipped)
+            nc.scalar.copy(out=tile[:].bitcast(F32).rearrange("p (c r u) -> p c r u", c=2, u=2),
+                           in_=banks[(name, n)][:].rearrange("p (c u r) -> p c r u", c=2, u=2))
             grouped[(name, n)] = tile
 
-        def quantise_input(name, n):
+        def quantise_tile(name, n):
             tile = grouped[(name, n)]
             if name == "k":
                 for c in range(2):
@@ -136,15 +134,15 @@ def tile_scaleddotproductattention_pa_kernel(tc, q, k, x, Wv, bv, out):
             else:
                 quantise(name, first_word(name, n, 0), 2 * P, tile[:])
 
-        warm_bank = psum.tile([P, BANK], F32, tag="short", name="warm_bank")
+        dummy_bank = psum.tile([P, BANK], F32, tag="back", name="dummy_bank")
 
-        def keep_warm(count):
-            for z in range(count):
-                nc.tensor.matmul(warm_bank[:], lhsT=ones[:], rhs=warm_rows[:], start=True, stop=True)
+        def dummy_matmuls(count):
+            for repeat in range(count):
+                nc.tensor.matmul(dummy_bank[:], lhsT=ones[:], rhs=dummy_rows[:], start=True, stop=True)
 
         def spread_bias():
             for half in range(2):
-                bank = psum.tile([P, BANK], F32, tag="short", name="bias_bank")
+                bank = psum.tile([P, BANK], F32, tag="back", name="bias_bank")
                 nc.tensor.matmul(bank[:], lhsT=ones[:], rhs=bias_row[:, half * BANK:(half + 1) * BANK],
                                  start=True, stop=True)
                 nc.vector.tensor_copy(
@@ -153,7 +151,7 @@ def tile_scaleddotproductattention_pa_kernel(tc, q, k, x, Wv, bv, out):
 
         def scores(i):
             for place, half in (("own", i // 4), ("other", 1 - i // 4)):
-                bank = psum.tile([P, BANK], F32, tag="long", name="scores")
+                bank = psum.tile([P, BANK], F32, tag="front", name="scores")
                 for c in range(2):
                     mx_pass(bank[:], "q", first_word("q", i, c), "k", first_word("k", 4 * half, c), BANK,
                             c == 0, c == 1)
@@ -168,8 +166,8 @@ def tile_scaleddotproductattention_pa_kernel(tc, q, k, x, Wv, bv, out):
             nc.vector.tensor_tensor(out=diag[:, 0:2 * P].rearrange("p (r a) -> p r a", a=2),
                                     in0=own[:, 2 * P * pair:2 * P * (pair + 1)].rearrange("p (a r) -> p r a", a=2),
                                     in1=pair_mask[i % 2][:].rearrange("p (r a) -> p r a", a=2), op=ALU.min)
-            nc.vector.tensor_reduce(out=diag[:, 2 * P + 1:2 * P + 2], in_=own[:, 2 * P * (1 - pair):2 * P * (2 - pair)],
-                                    axis=AX.X, op=ALU.max)
+            nc.vector.tensor_reduce(out=diag[:, 2 * P + 1:2 * P + 2],
+                                    in_=own[:, 2 * P * (1 - pair):2 * P * (2 - pair)], axis=AX.X, op=ALU.max)
             nc.vector.tensor_reduce(out=diag[:, 2 * P:2 * P + 1], in_=other[:], axis=AX.X, op=ALU.max)
             settle(1)
             nc.vector.tensor_scalar(out=scaled[:], in0=diag[:], scalar1=-1.0 / L, scalar2=None, op0=ALU.mult,
@@ -179,42 +177,25 @@ def tile_scaleddotproductattention_pa_kernel(tc, q, k, x, Wv, bv, out):
 
         def exponentials(i):
             half, pair = i // 4, (i % 4) // 2
-            row = e_rows[i]
-            for part, first, pairs, src in (
-                    (0, 2 * (1 - half), 2, banks[("other", i)][:]),
-                    (1, 2 * half + 1 - pair, 1, banks[("own", i)][:, 2 * P * (1 - pair):2 * P * (2 - pair)]),
-                    (2, 2 * half + pair, 1, grouped[("diag", i)][:, 0:2 * P])):
-                order = "p (u r a) -> p u r a" if part == 2 else "p (u a r) -> p u r a"
+            for part, first, pairs, src, order in (
+                    (0, 2 * (1 - half), 2, banks[("other", i)][:], "p (u a r) -> p u r a"),
+                    (1, 2 * half + 1 - pair, 1, banks[("own", i)][:, 2 * P * (1 - pair):2 * P * (2 - pair)],
+                     "p (u a r) -> p u r a"),
+                    (2, 2 * half + pair, 1, grouped[("diag", i)][:, 0:2 * P], "p (u r a) -> p u r a")):
+                columns = e_rows[i][:, 2 * P * first:2 * P * (first + pairs)]
                 nc.scalar.activation(
-                    out=row[:, 2 * P * first:2 * P * (first + pairs)].rearrange("p (u r a) -> p u r a", u=pairs, a=2),
+                    out=columns.rearrange("p (u r a) -> p u r a", u=pairs, a=2),
                     in_=src.rearrange(order, u=pairs, a=2), func=ACT.Exp, bias=grouped[("shift", i)][:],
                     scale=1.0 / L, accum_out=part_sums[:, 4 * i + part:4 * i + part + 1])
 
-        def row_scales(first, count):
-            part = slice(first, first + count)
-            nc.vector.tensor_reduce(out=row_sum[:, first:first + count],
-                                    in_=part_sums[:, 4 * first:4 * (first + count)].rearrange("p (i m) -> p i m", m=4)[:, :, 0:3],
+        def row_scales(i):
+            nc.vector.tensor_reduce(out=row_sum[:, i:i + 2],
+                                    in_=part_sums[:, 4 * i:4 * i + 8].rearrange("p (i m) -> p i m", m=4)[:, :, 0:3],
                                     axis=AX.X, op=ALU.add)
-            nc.vector.reciprocal(out=row_scale[:, first:first + count], in_=row_sum[:, first:first + count])
-
-        def flip_e(i):
-            bank = psum.tile([P, BANK], F32, tag="short", name="e_flipped")
-            pairs = e_rows[i][:].bitcast(F32)
-            for gu in range(4):
-                nc.tensor.transpose(bank[:, gu * P:(gu + 1) * P], pairs[:, gu * P:(gu + 1) * P], ident_f32[:])
-            banks[("e", i)] = bank
-
-        def regroup_e(i):
-            tile = to_quantise.tile([P, L], BF16, tag="grouped", name="e_grouped", align_bytes=64)
-            nc.scalar.copy(out=tile[:].bitcast(F32).rearrange("p (g i u) -> p g i u", g=2, u=2),
-                           in_=banks[("e", i)][:].rearrange("p (g u i) -> p g i u", g=2, u=2))
-            grouped[("e", i)] = tile
-
-        def quantise_e(i):
-            quantise("e", i * 2 * P, 2 * P, grouped[("e", i)][:])
+            nc.vector.reciprocal(out=row_scale[:, i:i + 2], in_=row_sum[:, i:i + 2])
 
         def v_bank(g, o):
-            bank = psum.tile([P, BANK], F32, tag="short", name="v_bank")
+            bank = psum.tile([P, BANK], F32, tag="back", name="v_bank")
             for t in range(4):
                 for c in range(2):
                     mx_pass(bank[:, t * P:(t + 1) * P], "x", first_word("x", 4 * g + t, c), "w", first_word("w", o, c),
@@ -235,12 +216,12 @@ def tile_scaleddotproductattention_pa_kernel(tc, q, k, x, Wv, bv, out):
             quantise("v", g * L + half * BANK, BANK, grouped[("v", g, half)][:])
 
         def out_bank(i, half):
-            bank = psum.tile([P, BANK], F32, tag="short", name="out_bank")
+            bank = psum.tile([P, BANK], F32, tag="back", name="out_bank")
             for g in range(2):
                 mx_pass(bank[:], "e", i * 2 * P + g * P, "v", g * L + half * BANK, BANK, g == 0, g == 1)
             banks[("out", i, half)] = bank
 
-        def out_store(i, half, on_vector):
+        def out_store(i, half, on_vector=False):
             tile = stores.tile([P, BANK], F32, tag="result", name="result")
             natural = tile[:].rearrange("p (o t) -> p o t", t=4)
             by_tile = banks[("out", i, half)][:].rearrange("p (t o) -> p o t", t=4)
@@ -251,99 +232,81 @@ def tile_scaleddotproductattention_pa_kernel(tc, q, k, x, Wv, bv, out):
                 nc.scalar.activation(out=natural, in_=by_tile, func=ACT.Copy, scale=row_scale[:, i:i + 1])
             nc.sync.dma_start(out=out_rows[:, i // 4, i % 4, half * BANK:(half + 1) * BANK], in_=tile[:])
 
-        waiting = []
-
-        settled = [0]
-
-        def settle(count):
-            for z in range(min(count, len(waiting) - settled[0])):
-                waiting[settled[0]]()
-                settled[0] += 1
-
-        def bring(tiles, ring, vector=()):
+        def bring(tiles):
             for name, n in tiles:
-                flip(name, n, ring)
+                flip(name, n, "front")
             for name, n in tiles:
-                regroup(name, n, on_vector=(name, n) in vector)
-                waiting.append(lambda name=name, n=n: quantise_input(name, n))
+                regroup(name, n)
+                waiting.append((quantise_tile, (name, n)))
 
-        def values(g, o, count=1):
-            v_bank(g, o)
-            v_regroup(g, o)
-            settle(count)
-            if o % 4 == 3:
-                waiting.append(lambda: quantise_v(g, o // 4))
-
-        plan = PLAN
-        keep_warm(WARM[0])
-        count = 0
-        for piece in plan:
-            if piece[0] in ("x", "w", "k", "q"):
-                count += 1
-            if piece[0] == "v":
-                settle(piece[3])
-                values(piece[1], piece[2], piece[4])
-            elif piece[0] == "b":
+        dummy_matmuls(DUMMIES_AT_START)
+        for idx, tile_name in enumerate(FIRST_TILES):
+            bring((tile_name,))
+            dummy_matmuls(1)
+            if idx == 2:
                 spread_bias()
-            elif piece[0] == "s":
-                settle(piece[1])
-            else:
-                bring([(piece[0], n) for n in piece[1]], piece[2], [(piece[0], n) for n in piece[3]])
-                if count < len(WARM):
-                    keep_warm(WARM[count])
+            if idx > 0:
+                settle(1)
+        settle(1)
+        dummy_matmuls(1)
+
+        for tiles, v_banks in GROUPS:
+            bring(tiles)
+            settle(2)
+            for g, o in v_banks:
+                v_bank(g, o)
+                v_regroup(g, o)
+                settle(2)
+                if (g, o) == (0, 3):
+                    waiting.append((quantise_v, (0, 0)))
+
         for s in range(TILES + 1):
-            settle(len(waiting) - settled[0] - (1 if s < TILES else 0))
+            settle(len(waiting) - (1 if s < TILES else 0))
             if s < TILES:
                 scores(s)
-            if 1 <= s:
-                v_bank((s - 1) // 4, 4 + (s - 1) % 4)
-            if 4 <= s:
-                out_bank(s - 4, 0)
-            fl = []
-            if 2 <= s:
-                flip_e(s - 2)
-            if s + 2 < TILES:
-                fl.append(("q", s + 2))
+            if s >= OUT_LAG:
+                out_bank(s - OUT_LAG, 0)
+            late = (s - 1) // 4, 4 + (s - 1) % 4
+            if s >= 1:
+                v_bank(late[0], late[1])
+            inputs = [("q", s + 2)] if s + 2 < TILES else []
             if s < 2:
-                fl.append(("w", 4 + 2 * s))
-                fl.append(("w", 5 + 2 * s))
-            for name, n in fl:
-                flip(name, n)
-            if 1 <= s <= TILES:
+                inputs += [("w", 4 + 2 * s), ("w", 5 + 2 * s)]
+            turned = ([("e", s - 2)] if s >= 2 else []) + inputs
+            for name, n in turned:
+                flip(name, n, "back")
+            if s >= 1:
                 exponentials(s - 1)
             if s < TILES:
                 row_max(s)
-            if 4 <= s:
-                out_store(s - 4, 0, False)
-            if 2 <= s:
-                regroup_e(s - 2)
-            for name, n in fl:
+            if s >= OUT_LAG:
+                out_store(s - OUT_LAG, 0)
+            for name, n in turned:
                 regroup(name, n)
-            if 1 <= s:
-                v_regroup((s - 1) // 4, 4 + (s - 1) % 4)
-            if s in (3, 5, 7, 8):
-                row_scales({3: 0, 5: 2, 7: 4, 8: 6}[s], 2)
-            for name, n in fl:
-                waiting.append(lambda name=name, n=n: quantise_input(name, n))
-            if s == 8:
-                waiting.append(lambda: quantise_v(1, 1))
-            if 2 <= s:
-                waiting.append(lambda s=s: quantise_e(s - 2))
-            if s == 4:
-                waiting.append(lambda: quantise_v(0, 1))
-        def finish(i, half, v):
+            if s >= 1:
+                v_regroup(late[0], late[1])
+            if s % 2 == 1 and s > 1:
+                row_scales(s - 3)
+            if s == TILES:
+                row_scales(s - 2)
+            for name, n in inputs:
+                waiting.append((quantise_tile, (name, n)))
+            if s % 4 == 0:
+                quarter = s // 4 + 1
+                waiting.append((quantise_v, (quarter % 2, quarter // 2)))
+            if s >= 2:
+                waiting.append((quantise_tile, ("e", s - 2)))
+
+        def finish(i, half, on_vector):
             out_bank(i, half)
-            out_store(i, half, v)
-        settle(9)
+            out_store(i, half, on_vector)
+
+        settle(len(waiting))
         finish(5, 0, False)
-        flip_e(7)
+        flip("e", 7, "back")
         finish(0, 1, True)
-        regroup_e(7)
+        regroup("e", 7)
         finish(1, 1, True)
-        quantise_e(7)
-        finish(6, 0, False)
-        for i in range(2, 6):
-            finish(i, 1, i % 2 == 1)
-        finish(7, 0, False)
-        finish(6, 1, True)
-        finish(7, 1, False)
+        quantise_tile("e", 7)
+        for idx, (i, half) in enumerate(((6, 0), (2, 1), (3, 1), (4, 1), (5, 1), (7, 0), (6, 1), (7, 1))):
+            finish(i, half, idx % 2 == 1)

from contextlib import ExitStack

import concourse.mybir as mybir
from concourse.masks import make_identity

FLOPS = 3 * 2 * 1024 * 1024 * 1024

F32 = mybir.dt.float32
BF16 = mybir.dt.bfloat16
U32 = mybir.dt.uint32
U8 = mybir.dt.uint8
FP8X4 = mybir.dt.float8_e4m3fn_x4
ALU = mybir.AluOpType
ACT = mybir.ActivationFunctionType
AX = mybir.AxisListType

P = 128
L = 1024
TILES = L // P
BANK = 512
MASKED = -3.4028234663852886e38

LOADS = (("x", 0, 1), ("x", 1, 1), ("x", 2, 1), ("x", 3, 1), ("w", 0, 1), ("w", 1, 1), ("w", 2, 2), ("x", 4, 2),
         ("x", 6, 2), ("k", 0, 2), ("k", 2, 2), ("k", 4, 2), ("q", 0, 2), ("k", 6, 2), ("w", 4, 2), ("q", 2, 2),
         ("w", 6, 2), ("q", 4, 4))

FIRST_TILES = (("x", 0), ("x", 1), ("x", 2), ("x", 3), ("w", 0), ("w", 1))
GROUPS = (((("w", 2), ("w", 3), ("x", 4), ("x", 5)), ((0, 0), (0, 1))),
          ((("x", 6), ("x", 7), ("k", 0), ("k", 1)), ((0, 2), (0, 3))),
          ((("k", 2), ("k", 3), ("k", 4), ("k", 5)), ((1, 0), (1, 1))),
          ((("q", 0), ("k", 6), ("k", 7), ("q", 1)), ((1, 2), (1, 3))))
DUMMIES_AT_START = 4
OUT_LAG = 4


def tile_scaleddotproductattention_pa_kernel(tc, q, k, x, Wv, bv, out):
    nc = tc.nc
    with ExitStack() as ctx:
        const = ctx.enter_context(tc.tile_pool(name="const", bufs=1))
        keep = ctx.enter_context(tc.tile_pool(name="keep", bufs=1))
        to_quantise = ctx.enter_context(tc.tile_pool(name="to_quantise", bufs=10))
        v_to_quantise = ctx.enter_context(tc.tile_pool(name="v_to_quantise", bufs=2))
        small = ctx.enter_context(tc.tile_pool(name="small", bufs=3))
        stores = ctx.enter_context(tc.tile_pool(name="stores", bufs=12))
        psum = ctx.enter_context(tc.psum_pool(name="psum", bufs=4))
        ctx.enter_context(tc.manual_schedule())

        ident = const.tile([P, P], F32, name="ident")
        diag_mask = const.tile([P, P], F32, name="diag_mask")
        pair_mask = [const.tile([P, 2 * P], F32, name="pair_mask%d" % a) for a in range(2)]
        ones = const.tile([P, P], BF16, name="ones")
        dummy_rows = const.tile([P, BANK], BF16, name="dummy_rows")
        bias_row = const.tile([P, L], BF16, name="bias_row")
        bias = const.tile([P, L], F32, name="bias")
        part_sums = const.tile([P, 4 * TILES], F32, name="part_sums")
        row_sum = const.tile([P, TILES], F32, name="row_sum")
        row_scale = const.tile([P, TILES], F32, name="row_scale")

        nc.vector.memset(bias_row[:], 0.0)
        nc.scalar.dma_start(out=bias_row[0:1, :], in_=bv.rearrange("(o n) -> o n", o=1))
        nc.vector.memset(ones[:], 1.0)
        nc.vector.memset(dummy_rows[:], 1.0)
        make_identity(nc, ident[:])
        nc.vector.tensor_scalar(out=diag_mask[:], in0=ident[:], scalar1=-2.0, scalar2=1.0,
                                op0=ALU.mult, op1=ALU.add)
        nc.vector.tensor_scalar(out=diag_mask[:], in0=diag_mask[:], scalar1=-MASKED, scalar2=0.0,
                                op0=ALU.mult, op1=ALU.add)
        for a in range(2):
            nc.vector.memset(pair_mask[a][:], -MASKED)
            nc.vector.tensor_copy(out=pair_mask[a][:].rearrange("p (r a) -> p a r", a=2)[:, a, :], in_=diag_mask[:])

        raw = {}
        words = {}
        scales = {}
        for name in ("k", "q", "x", "w", "v", "e"):
            if name in ("k", "q", "x", "w"):
                raw[name] = keep.tile([P, TILES * L], BF16, name="raw_" + name)
            words[name] = keep.tile([P, 2 * L], U32, name="words_" + name, align_bytes=64)
            scales[name] = keep.tile([P, 2 * L], U8, name="scales_" + name, align_bytes=64)
        e_rows = [keep.tile([P, L], BF16, name="e_rows%d" % i) for i in range(TILES)]

        dram = {"w": Wv.rearrange("(g p t) h -> p g t h", g=2, p=P, t=4)}
        for name, src in (("k", k), ("q", q), ("x", x)):
            dram[name] = src.flatten_outer_dims().rearrange("(g p t) h -> p g t h", g=2, p=P, t=4)
        for name, n0, count in LOADS:
            nc.sync.dma_start(out=raw[name][:, n0 * L:(n0 + count) * L].rearrange("p (n h) -> p n h", n=count),
                              in_=dram[name][:, n0 // 4, n0 % 4:n0 % 4 + count, :])
        out_rows = out.flatten_outer_dims().rearrange("(g p t) o -> p g t o", g=2, p=P, t=4)

        def first_word(name, n, c):
            if name == "k":
                return c * L + n * P
            return n * 2 * P + c * P

        def quantise(name, start, count, values):
            nc.vector.quantize_mx(out=words[name][:, start:start + count].bitcast(FP8X4),
                                  scales=scales[name][:, start:start + count], in_=values)

        def mx_pass(acc, stationary, s_start, moving, m_start, n, first, last):
            nc.tensor.matmul_mx(out=acc,
                                lhsT=words[stationary][:, s_start:s_start + P].bitcast(FP8X4),
                                lhsT_scale=scales[stationary][:, s_start:s_start + P],
                                rhs=words[moving][:, m_start:m_start + n].bitcast(FP8X4),
                                rhs_scale=scales[moving][:, m_start:m_start + n],
                                start=first, stop=last)

        banks = {}
        grouped = {}
        waiting = []

        def settle(count):
            for function, arguments in waiting[:count]:
                function(*arguments)
            waiting[:count] = []

        def flip(name, n, ring):
            bank = psum.tile([P, BANK], F32, tag=ring, name="flipped")
            pairs = e_rows[n][:].bitcast(F32) if name == "e" else raw[name][:, n * L:(n + 1) * L].bitcast(F32)
            for cu in range(4):
                nc.tensor.transpose(bank[:, cu * P:(cu + 1) * P], pairs[:, cu * P:(cu + 1) * P], ident[:])
            banks[(name, n)] = bank

        def regroup(name, n):
            tile = to_quantise.tile([P, L], BF16, tag="grouped", name="grouped", align_bytes=64)
            nc.scalar.copy(out=tile[:].bitcast(F32).rearrange("p (c r u) -> p c r u", c=2, u=2),
                           in_=banks[(name, n)][:].rearrange("p (c u r) -> p c r u", c=2, u=2))
            grouped[(name, n)] = tile

        def quantise_tile(name, n):
            tile = grouped[(name, n)]
            if name == "k":
                for c in range(2):
                    quantise(name, first_word(name, n, c), P, tile[:, c * BANK:(c + 1) * BANK])
            else:
                quantise(name, first_word(name, n, 0), 2 * P, tile[:])

        dummy_bank = psum.tile([P, BANK], F32, tag="back", name="dummy_bank")

        def dummy_matmuls(count):
            for repeat in range(count):
                nc.tensor.matmul(dummy_bank[:], lhsT=ones[:], rhs=dummy_rows[:], start=True, stop=True)

        def spread_bias():
            for half in range(2):
                bank = psum.tile([P, BANK], F32, tag="back", name="bias_bank")
                nc.tensor.matmul(bank[:], lhsT=ones[:], rhs=bias_row[:, half * BANK:(half + 1) * BANK],
                                 start=True, stop=True)
                nc.vector.tensor_copy(
                    out=bias[:, half * BANK:(half + 1) * BANK].rearrange("p (t o) -> p t o", t=4),
                    in_=bank[:].rearrange("p (o t) -> p t o", t=4))

        def scores(i):
            for place, half in (("own", i // 4), ("other", 1 - i // 4)):
                bank = psum.tile([P, BANK], F32, tag="front", name="scores")
                for c in range(2):
                    mx_pass(bank[:], "q", first_word("q", i, c), "k", first_word("k", 4 * half, c), BANK,
                            c == 0, c == 1)
                banks[(place, i)] = bank

        def row_max(i):
            diag = small.tile([P, 2 * P + 2], F32, tag="diag", name="diag")
            scaled = small.tile([P, 2 * P + 2], F32, tag="scaled", name="scaled")
            shift = small.tile([P, 1], F32, tag="shift", name="shift")
            own, other = banks[("own", i)], banks[("other", i)]
            pair = (i % 4) // 2
            nc.vector.tensor_tensor(out=diag[:, 0:2 * P].rearrange("p (r a) -> p r a", a=2),
                                    in0=own[:, 2 * P * pair:2 * P * (pair + 1)].rearrange("p (a r) -> p r a", a=2),
                                    in1=pair_mask[i % 2][:].rearrange("p (r a) -> p r a", a=2), op=ALU.min)
            nc.vector.tensor_reduce(out=diag[:, 2 * P + 1:2 * P + 2],
                                    in_=own[:, 2 * P * (1 - pair):2 * P * (2 - pair)], axis=AX.X, op=ALU.max)
            nc.vector.tensor_reduce(out=diag[:, 2 * P:2 * P + 1], in_=other[:], axis=AX.X, op=ALU.max)
            settle(1)
            nc.vector.tensor_scalar(out=scaled[:], in0=diag[:], scalar1=-1.0 / L, scalar2=None, op0=ALU.mult,
                                    op1=ALU.min, accum_out=shift[:])
            grouped[("diag", i)] = diag
            grouped[("shift", i)] = shift

        def exponentials(i):
            half, pair = i // 4, (i % 4) // 2
            for part, first, pairs, src, order in (
                    (0, 2 * (1 - half), 2, banks[("other", i)][:], "p (u a r) -> p u r a"),
                    (1, 2 * half + 1 - pair, 1, banks[("own", i)][:, 2 * P * (1 - pair):2 * P * (2 - pair)],
                     "p (u a r) -> p u r a"),
                    (2, 2 * half + pair, 1, grouped[("diag", i)][:, 0:2 * P], "p (u r a) -> p u r a")):
                columns = e_rows[i][:, 2 * P * first:2 * P * (first + pairs)]
                nc.scalar.activation(
                    out=columns.rearrange("p (u r a) -> p u r a", u=pairs, a=2),
                    in_=src.rearrange(order, u=pairs, a=2), func=ACT.Exp, bias=grouped[("shift", i)][:],
                    scale=1.0 / L, accum_out=part_sums[:, 4 * i + part:4 * i + part + 1])

        def row_scales(i):
            nc.vector.tensor_reduce(out=row_sum[:, i:i + 2],
                                    in_=part_sums[:, 4 * i:4 * i + 8].rearrange("p (i m) -> p i m", m=4)[:, :, 0:3],
                                    axis=AX.X, op=ALU.add)
            nc.vector.reciprocal(out=row_scale[:, i:i + 2], in_=row_sum[:, i:i + 2])

        def v_bank(g, o):
            bank = psum.tile([P, BANK], F32, tag="back", name="v_bank")
            for t in range(4):
                for c in range(2):
                    mx_pass(bank[:, t * P:(t + 1) * P], "x", first_word("x", 4 * g + t, c), "w", first_word("w", o, c),
                            P, c == 0, c == 1)
            banks[("v", g, o)] = bank

        def v_regroup(g, o):
            if o % 4 == 0:
                grouped[("v", g, o // 4)] = v_to_quantise.tile([P, 4 * BANK], BF16, tag="v_grouped", name="v_grouped",
                                                               align_bytes=64)
            nc.vector.tensor_tensor(
                out=grouped[("v", g, o // 4)][:, (o % 4) * BANK:(o % 4 + 1) * BANK].rearrange("p (o t) -> p o t", t=4),
                in0=banks[("v", g, o)][:].rearrange("p (t o) -> p o t", t=4),
                in1=bias[:, o * P:(o + 1) * P].unsqueeze(2).to_broadcast([P, P, 4]),
                op=ALU.add)

        def quantise_v(g, half):
            quantise("v", g * L + half * BANK, BANK, grouped[("v", g, half)][:])

        def out_bank(i, half):
            bank = psum.tile([P, BANK], F32, tag="back", name="out_bank")
            for g in range(2):
                mx_pass(bank[:], "e", i * 2 * P + g * P, "v", g * L + half * BANK, BANK, g == 0, g == 1)
            banks[("out", i, half)] = bank

        def out_store(i, half, on_vector=False):
            tile = stores.tile([P, BANK], F32, tag="result", name="result")
            natural = tile[:].rearrange("p (o t) -> p o t", t=4)
            by_tile = banks[("out", i, half)][:].rearrange("p (t o) -> p o t", t=4)
            if on_vector:
                nc.vector.tensor_scalar(out=natural, in0=by_tile, scalar1=row_scale[:, i:i + 1], scalar2=None,
                                        op0=ALU.mult)
            else:
                nc.scalar.activation(out=natural, in_=by_tile, func=ACT.Copy, scale=row_scale[:, i:i + 1])
            nc.sync.dma_start(out=out_rows[:, i // 4, i % 4, half * BANK:(half + 1) * BANK], in_=tile[:])

        def bring(tiles):
            for name, n in tiles:
                flip(name, n, "front")
            for name, n in tiles:
                regroup(name, n)
                waiting.append((quantise_tile, (name, n)))

        dummy_matmuls(DUMMIES_AT_START)
        for idx, tile_name in enumerate(FIRST_TILES):
            bring((tile_name,))
            dummy_matmuls(1)
            if idx == 2:
                spread_bias()
            if idx > 0:
                settle(1)
        settle(1)
        dummy_matmuls(1)

        for tiles, v_banks in GROUPS:
            bring(tiles)
            settle(2)
            for g, o in v_banks:
                v_bank(g, o)
                v_regroup(g, o)
                settle(2)
                if (g, o) == (0, 3):
                    waiting.append((quantise_v, (0, 0)))

        for s in range(TILES + 1):
            settle(len(waiting) - (1 if s < TILES else 0))
            if s < TILES:
                scores(s)
            if s >= OUT_LAG:
                out_bank(s - OUT_LAG, 0)
            late = (s - 1) // 4, 4 + (s - 1) % 4
            if s >= 1:
                v_bank(late[0], late[1])
            inputs = [("q", s + 2)] if s + 2 < TILES else []
            if s < 2:
                inputs += [("w", 4 + 2 * s), ("w", 5 + 2 * s)]
            turned = ([("e", s - 2)] if s >= 2 else []) + inputs
            for name, n in turned:
                flip(name, n, "back")
            if s >= 1:
                exponentials(s - 1)
            if s < TILES:
                row_max(s)
            if s >= OUT_LAG:
                out_store(s - OUT_LAG, 0)
            for name, n in turned:
                regroup(name, n)
            if s >= 1:
                v_regroup(late[0], late[1])
            if s % 2 == 1 and s > 1:
                row_scales(s - 3)
            if s == TILES:
                row_scales(s - 2)
            for name, n in inputs:
                waiting.append((quantise_tile, (name, n)))
            if s % 4 == 0:
                quarter = s // 4 + 1
                waiting.append((quantise_v, (quarter % 2, quarter // 2)))
            if s >= 2:
                waiting.append((quantise_tile, ("e", s - 2)))

        def finish(i, half, on_vector):
            out_bank(i, half)
            out_store(i, half, on_vector)

        settle(len(waiting))
        finish(5, 0, False)
        flip("e", 7, "back")
        finish(0, 1, True)
        regroup("e", 7)
        finish(1, 1, True)
        quantise_tile("e", 7)
        for idx, (i, half) in enumerate(((6, 0), (2, 1), (3, 1), (4, 1), (5, 1), (7, 0), (6, 1), (7, 1))):
            finish(i, half, idx % 2 == 1)
